import numpy as np
import ml_dtypes


def mxq(x, axis, fmt="e4m3"):
    dtype, down = {"e4m3": (ml_dtypes.float8_e4m3fn, 7), "e5m2": (ml_dtypes.float8_e5m2, 14)}[fmt]
    v = np.moveaxis(np.asarray(x, np.float32).astype(ml_dtypes.bfloat16).astype(np.float64), axis, -1)
    blocks = v.reshape(v.shape[:-1] + (-1, 32))
    amax = np.abs(blocks).max(-1, keepdims=True)
    byte = np.maximum(np.where(amax > 0, np.frexp(amax)[1] - 1 + 127, 0) - down, 1)
    scale = np.exp2(byte - 127.0)
    codes = (blocks / scale).astype(np.float32).astype(dtype).astype(np.float64)
    return np.moveaxis((codes * scale).reshape(v.shape), -1, axis)


WIDE = False


def mx_kscale(k):
    if not WIDE:
        return np.ones(k)
    levels = np.array([10, -10, 5, -5, 0])
    if k % 512:
        return np.exp2(np.random.permutation(np.resize(levels, k // 32))).repeat(32)
    a = np.empty((k // 512, 16))
    for p in range(k // 512):
        a[p, :8] = np.random.permutation(np.resize(levels, 8))
        for g in range(8):
            far = levels[np.abs(levels - a[p, g]) >= 10]
            a[p, g + 8] = far[np.random.randint(len(far))]
    return np.exp2(a.ravel()).repeat(32)


BF16 = ml_dtypes.bfloat16


def bf(x):
    return np.asarray(x, np.float32).astype(BF16)


def f64(x):
    return np.asarray(x).astype(np.float64)


B, HD, NH, H, W, F = 2, 512, 4, 32, 64, 2048
HEAD = HD // NH
P = H * W


def rms_in(x, w, eps=1e-8):
    std = np.std(x, axis=(-2, -1), keepdims=True, ddof=1)
    return x / (std + eps) * w[None, :, None, None]


def setup_inputs():
    n = np.random.standard_normal
    s = mx_kscale(HD)

    def stream():
        return n((B, NH, H, W, HEAD)) * 0.35 * (0.5 + np.random.random((B, NH, 1, 1, HEAD))) + 0.5 * n((B, NH, 1, 1, HEAD))

    return {"xx": bf(stream()), "xy": bf(stream()),
            "x": bf(n((B, HD, H, W)) * (0.5 + np.random.random((B, HD, 1, 1))) + 0.5 * n((B, HD, 1, 1))),
            "norm2_w": bf((1.0 + 0.1 * n(HD)) * s),
            "out_w": bf(n((HD, HD)) / np.sqrt(HD) / s[None, :]),
            "out_b": bf(0.1 * n(HD)),
            "gamma_att": bf(0.5 + 0.2 * n(HD))}


def reference(xx, xy, x, norm2_w, out_w, out_b, gamma_att):
    a = (f64(xx) + f64(xy)) * 0.5
    a = a.transpose(0, 1, 4, 2, 3).reshape(B, HD, H, W)
    a = rms_in(a, f64(norm2_w)).reshape(B, HD, P)
    a = (mxq(f64(out_w), 1, "e4m3") @ mxq(a, 1, "e4m3")) + f64(out_b)[None, :, None]
    return a.reshape(B, HD, H, W) * f64(gamma_att)[None, :, None, None] + f64(x)

@@ -1,0 +1,307 @@
+from contextlib import ExitStack
+
+import concourse.mybir as mybir
+from concourse.masks import make_identity
+
+F32 = mybir.dt.float32
+BF16 = mybir.dt.bfloat16
+U32 = mybir.dt.uint32
+U8 = mybir.dt.uint8
+FP8X4 = mybir.dt.float8_e4m3fn_x4
+ALU = mybir.AluOpType
+ACT = mybir.ActivationFunctionType
+AX = mybir.AxisListType
+
+P = 128
+B = 2
+NH = 4
+HEAD = 128
+HD = NH * HEAD
+T = 4
+POS = 32 * 64
+PART = 1024
+PARTS = POS // PART
+RUN = PART // P
+CHUNK = 512
+CHUNKS = POS // CHUNK
+CPP = PART // CHUNK
+TILES = CHUNK // P
+OT = HD // P
+EPS = 1e-8
+
+FLOPS = 2 * B * HD * HD * POS
+
+
+def tile_axialattentionblock_pb_t_kernel(tc, xx, xy, x, norm2_w, out_w, out_b, gamma_att, out):
+    nc = tc.nc
+    by_partition = "b n (q hp) (wp i) c -> b q n (hp wp) i c"
+    xx_v = xx.rearrange(by_partition, q=PARTS, i=RUN)
+    xy_v = xy.rearrange(by_partition, q=PARTS, i=RUN)
+    x_v = x.rearrange("b (m p) h w -> b m p (h w)", p=P)
+    out_v = out.rearrange("b (m p) h w -> b m p (h w)", p=P)
+
+    with ExitStack() as ctx:
+        const = ctx.enter_context(tc.tile_pool(name="const", bufs=1))
+        stream = ctx.enter_context(tc.tile_pool(name="stream", bufs=B * PARTS))
+        xpool = ctx.enter_context(tc.tile_pool(name="xpool", bufs=OT))
+        respool = ctx.enter_context(tc.tile_pool(name="respool", bufs=6))
+        sums_pool = ctx.enter_context(tc.tile_pool(name="sums", bufs=2))
+        big = ctx.enter_context(tc.tile_pool(name="big", bufs=2))
+        junk = ctx.enter_context(tc.tile_pool(name="junk", bufs=1))
+        work = ctx.enter_context(tc.tile_pool(name="work", bufs=3))
+        psum = ctx.enter_context(tc.psum_pool(name="psum", bufs=8))
+
+        ident = const.tile([P, P], F32)
+        make_identity(nc, ident[:])
+        ident_bf = const.tile([P, P], BF16)
+        nc.vector.tensor_copy(out=ident_bf[:], in_=ident[:])
+
+        one = const.tile([P, 1], F32)
+        nc.vector.memset(one[:], 1.0)
+        one_root = const.tile([P, 1], F32)
+        nc.scalar.activation(out=one_root[:], in_=one[:], func=ACT.Sqrt)
+
+        stream_of = {}
+
+        def load_part(b, q):
+            tiles = []
+            for name, view in (("xy", xy_v), ("xx", xx_v)):
+                t_sb = stream.tile([P, RUN, HD], BF16, tag=name, name="%s_%d_%d" % (name, b, q))
+                for n in range(NH):
+                    nc.sync.dma_start(out=t_sb[:, :, n * HEAD : (n + 1) * HEAD], in_=view[b, q, n])
+                tiles.append(t_sb)
+            stream_of[(b, q)] = tiles
+
+        x_of = {}
+
+        def load_x(b, m):
+            x_sb = xpool.tile([P, POS], BF16, tag="x", name="x_%d_%d" % (b, m))
+            nc.sync.dma_start(out=x_sb[:], in_=x_v[b, m])
+            x_of[(b, m)] = x_sb
+
+        load_part(0, 0)
+        vec_rows = const.tile([P, P], BF16)
+        nc.vector.memset(vec_rows[:], 0.0)
+        nc.scalar.dma_start(out=vec_rows[0:OT, :], in_=out_b.rearrange("(n c) -> n c", c=P))
+        nc.scalar.dma_start(out=vec_rows[OT : 2 * OT, :], in_=gamma_att.rearrange("(n c) -> n c", c=P))
+        norm_rows = const.tile([P, T], BF16)
+        nc.scalar.dma_start(out=norm_rows[:], in_=norm2_w.rearrange("(p t) -> p t", t=T))
+        w_rows = const.tile([P, OT, HD], BF16)
+        load_part(0, 1)
+        nc.sync.dma_start(out=w_rows[:], in_=out_w.rearrange("(m p) j -> p m j", p=P))
+        for m in range(OT):
+            load_x(0, m)
+        load_part(1, 0)
+        load_part(1, 1)
+
+        vecs = const.tile([P, 2 * OT], F32)
+        gamma = vecs[:, OT : 2 * OT]
+        half_w = const.tile([P, T], F32)
+        bias_gamma = const.tile([P, OT], F32)
+
+        def prepare_vectors():
+            vec_ps = psum.tile([P, P], BF16, tag="bank")
+            nc.tensor.transpose(vec_ps[:], vec_rows[:], ident_bf[:])
+            nc.vector.tensor_copy(out=vecs[:], in_=vec_ps[:, 0 : 2 * OT])
+            nc.vector.tensor_scalar_mul(out=half_w[:], in0=norm_rows[:], scalar1=0.5)
+            nc.vector.tensor_tensor(out=bias_gamma[:], in0=vecs[:, 0:OT], in1=gamma, op=ALU.mult)
+
+        w_grouped = const.tile([P, HD, T], BF16, align_bytes=64)
+        w_codes = const.tile([P, HD], U32, align_bytes=64)
+        w_scales = const.tile([P, HD], U8, align_bytes=64)
+
+        def quantise_weights():
+            words = w_rows[:].rearrange("p m j -> p (m j)").bitcast(F32)
+            grouped_words = w_grouped[:].rearrange("k o t -> k (o t)").bitcast(F32)
+            half = HD // T * 2
+            for h in range(2):
+                wT = psum.tile([P, 2, 2, P], F32, tag="bank")
+                for d in range(2):
+                    m = 2 * h + d
+                    for u in range(2):
+                        nc.tensor.transpose(wT[:, d, u, :], words[:, m * half + u : (m + 1) * half : 2], ident[:])
+                nc.vector.tensor_copy(
+                    out=grouped_words[:, h * 2 * half : (h + 1) * 2 * half].rearrange("k (d o u) -> k d o u", d=2, u=2),
+                    in_=wT[:].rearrange("k d u o -> k d o u"),
+                )
+            nc.vector.quantize_mx(
+                out=w_codes[:].bitcast(FP8X4), scales=w_scales[:], in_=w_grouped[:].rearrange("k o t -> k (o t)")
+            )
+
+        sT_of = {}
+        sums_of = {}
+        std_of = {}
+        r_of = {}
+        res_of = {}
+        scaled_of = {}
+        codes_of = {}
+
+        def sum_unit(b, g, u):
+            if g == 0 and u == 0:
+                sT_of[b] = big.tile([P, T, POS], F32, tag="sT", name="sT%d" % b)
+                sums_of[b] = (
+                    sums_pool.tile([P, T, CHUNKS], F32, tag="sums", name="sums%d" % b),
+                    sums_pool.tile([P, T, CHUNKS], F32, tag="sumsq", name="sumsq%d" % b),
+                )
+            q, h = divmod(g, CPP)
+            xy_sb, xx_sb = stream_of[(b, q)]
+            banks = []
+            for name, t_sb in (("xyT", xy_sb), ("xxT", xx_sb)):
+                words = t_sb[:].rearrange("p i j -> p (i j)").bitcast(F32)
+                bank = psum.tile([P, TILES, P], F32, tag="bank", name="%s_%d_%d_%d" % (name, b, g, u))
+                for i in range(TILES):
+                    first = (h * TILES + i) * (HD // 2)
+                    nc.tensor.transpose(bank[:, i, :], words[:, first + u : first + HD // 2 : 2], ident[:])
+                banks.append(bank)
+            xyT_sb = work.tile([P, CHUNK], F32, tag="xyT_sb")
+            nc.scalar.copy(out=xyT_sb[:], in_=banks[0][:].rearrange("c i p -> c (i p)"))
+            xy_pairs = xyT_sb[:].bitcast(BF16).rearrange("c (w e) -> c e w", e=2)
+            xx_pairs = banks[1][:].rearrange("c i p -> c (i p)").bitcast(BF16).rearrange("c (w e) -> c e w", e=2)
+            for e in range(2):
+                t = 2 * u + e
+                nc.vector.scalar_tensor_tensor(
+                    out=sT_of[b][:, t, g * CHUNK : (g + 1) * CHUNK],
+                    in0=xx_pairs[:, e, :],
+                    scalar=1.0,
+                    in1=xy_pairs[:, e, :],
+                    op0=ALU.mult,
+                    op1=ALU.add,
+                    accum_out=sums_of[b][0][:, t, g : g + 1],
+                )
+
+        def square_unit(b, g, u):
+            for e in range(2):
+                t = 2 * u + e
+                squares = junk.tile([P, CHUNK], BF16, tag="squares")
+                nc.scalar.activation(
+                    out=squares[:],
+                    in_=sT_of[b][:, t, g * CHUNK : (g + 1) * CHUNK],
+                    func=ACT.Square,
+                    accum_out=sums_of[b][1][:, t, g : g + 1],
+                )
+
+        def deviation(b):
+            sums, sumsq = sums_of[b]
+            sum_s = sums_pool.tile([P, T], F32, tag="sum_s")
+            nc.vector.tensor_reduce(out=sum_s[:], in_=sums[:], axis=AX.X, op=ALU.add)
+            sum_q = sums_pool.tile([P, T], F32, tag="sum_q")
+            nc.vector.tensor_reduce(out=sum_q[:], in_=sumsq[:], axis=AX.X, op=ALU.add)
+            sum_s2 = sums_pool.tile([P, T], F32, tag="sum_s2")
+            nc.vector.scalar_tensor_tensor(
+                out=sum_s2[:], in0=sum_s[:], scalar=-1.0 / POS, in1=sum_s[:], op0=ALU.mult, op1=ALU.mult
+            )
+            centred = sums_pool.tile([P, T], F32, tag="centred")
+            nc.vector.tensor_tensor(out=centred[:], in0=sum_s2[:], in1=sum_q[:], op=ALU.add)
+            var = sums_pool.tile([P, T], F32, tag="var")
+            nc.vector.tensor_scalar(
+                out=var[:], in0=centred[:], scalar1=0.25 / (POS - 1), scalar2=0.0, op0=ALU.mult, op1=ALU.max
+            )
+            std = sums_pool.tile([P, T], F32, tag="std")
+            nc.scalar.activation(out=std[:], in_=var[:], func=ACT.Sqrt)
+            std_of[b] = std
+
+        def scale_factors(b):
+            den = sums_pool.tile([P, T], F32, tag="den")
+            nc.vector.tensor_scalar_add(out=den[:], in0=std_of[b][:], scalar1=EPS)
+            inv = sums_pool.tile([P, T], F32, tag="inv")
+            nc.vector.reciprocal(out=inv[:], in_=den[:])
+            r = sums_pool.tile([P, T], F32, tag="r")
+            nc.vector.tensor_tensor(out=r[:], in0=inv[:], in1=half_w[:], op=ALU.mult)
+            r_of[b] = r
+
+        def residual_part(b, q, m):
+            res = respool.tile([P, PART], F32, tag="res", name="res%d%d%d" % (b, q, m))
+            nc.gpsimd.tensor_scalar(
+                out=res[:],
+                in0=x_of[(b, m)][:, q * PART : (q + 1) * PART],
+                scalar1=1.0,
+                scalar2=bias_gamma[:, m : m + 1],
+                op0=ALU.mult,
+                op1=ALU.add,
+            )
+            res_of[(b, q, m)] = res
+
+        def scale_chunk(b, g):
+            scaled = work.tile([P, T, CHUNK], BF16, tag="scaled")
+            for t in range(T):
+                part = sT_of[b][:, t, g * CHUNK : (g + 1) * CHUNK]
+                if t % 2 == 0:
+                    nc.scalar.activation(out=scaled[:, t, :], in_=part, func=ACT.Copy, scale=r_of[b][:, t : t + 1])
+                else:
+                    nc.gpsimd.tensor_scalar(
+                        out=scaled[:, t, :], in0=part, scalar1=r_of[b][:, t : t + 1], scalar2=0.0, op0=ALU.mult, op1=ALU.add
+                    )
+            scaled_of[(b, g)] = scaled
+
+        def quantise_chunk(b, g):
+            grouped = work.tile([P, CHUNK, T], BF16, tag="grouped", align_bytes=64)
+            nc.vector.tensor_copy(
+                out=grouped[:].rearrange("c (q i) t -> c q t i", i=4),
+                in_=scaled_of[(b, g)][:].rearrange("c t (q i) -> c q t i", i=4),
+            )
+            g_codes = work.tile([P, CHUNK], U32, tag="g_codes", align_bytes=64)
+            g_scales = work.tile([P, CHUNK], U8, tag="g_scales", align_bytes=64)
+            nc.vector.quantize_mx(
+                out=g_codes[:].bitcast(FP8X4), scales=g_scales[:], in_=grouped[:].rearrange("c p t -> c (p t)")
+            )
+            codes_of[(b, g)] = (g_codes, g_scales)
+
+        def finish_chunk(b, g):
+            q, h = divmod(g, CPP)
+            g_codes, g_scales = codes_of[(b, g)]
+            acc_of = {}
+            for m in range(OT):
+                acc = psum.tile([P, CHUNK], F32, tag="bank")
+                nc.tensor.matmul_mx(
+                    out=acc[:],
+                    lhsT=w_codes[:, m * P : (m + 1) * P].bitcast(FP8X4),
+                    lhsT_scale=w_scales[:, m * P : (m + 1) * P],
+                    rhs=g_codes[:].bitcast(FP8X4),
+                    rhs_scale=g_scales[:],
+                    start=True,
+                    stop=True,
+                )
+                acc_of[m] = acc
+            for m in range(OT):
+                res = res_of[(b, q, m)][:].rearrange("o (p r) -> o p r", r=RUN)[:, :, h * TILES : (h + 1) * TILES]
+                nc.vector.scalar_tensor_tensor(
+                    out=res,
+                    in0=acc_of[m][:].rearrange("o (i p) -> o p i", i=TILES),
+                    scalar=gamma[:, m : m + 1],
+                    in1=res,
+                    op0=ALU.mult,
+                    op1=ALU.add,
+                )
+                if h == CPP - 1:
+                    nc.sync.dma_start(out=out_v[b, m][:, q * PART : (q + 1) * PART], in_=res_of[(b, q, m)][:])
+
+        units = [(b, g, u) for b in range(B) for g in range(CHUNKS) for u in range(2)]
+        per_batch = CHUNKS * 2
+        for s in range(len(units) + 2 * CHUNKS + 4):
+            if s < len(units):
+                sum_unit(*units[s])
+            if s == 1:
+                prepare_vectors()
+            if s == 3:
+                quantise_weights()
+            if 0 < s <= len(units):
+                square_unit(*units[s - 1])
+            for b in range(B):
+                k = s - per_batch * (b + 1)
+                if k == 0:
+                    deviation(b)
+                if k == 1:
+                    scale_factors(b)
+                if k >= 1 and (k - 1) % 2 == 0 and (k - 1) // 2 < CHUNKS:
+                    c = (k - 1) // 2
+                    scale_chunk(b, c)
+                    if c % CPP == 0:
+                        for m in range(OT):
+                            residual_part(b, c // CPP, m)
+                if k >= 2 and (k - 2) % 2 == 0 and (k - 2) // 2 < CHUNKS:
+                    quantise_chunk(b, (k - 2) // 2)
+                if k >= 3 and (k - 3) % 2 == 0 and (k - 3) // 2 < CHUNKS:
+                    finish_chunk(b, (k - 3) // 2)
+                    if b == 0 and (k - 3) // 2 == CHUNKS - 1:
+                        for m in range(OT):
+                            load_x(1, m)

@@ -18,6 +18,7 @@ NH = 4
 HEAD = 128
 HD = NH * HEAD
 T = 4
+U = 2
 POS = 32 * 64
 PART = 1024
 PARTS = POS // PART
@@ -28,33 +29,40 @@ CPP = PART // CHUNK
 TILES = CHUNK // P
 OT = HD // P
 EPS = 1e-8
+SCALERS = ("GGGGGGGGGGGGGGGG", "GGSGGGSGGGSGGGSG")
+GROUPERS = ("SSSS", "SSSS")
+SUMMED = ((0, 0, 0), (0, 0, 1), (0, 1, 0))
+LEAVERS = "VSVV"
 
 FLOPS = 2 * B * HD * HD * POS
 
 
 def tile_axialattentionblock_pb_t_kernel(tc, xx, xy, x, norm2_w, out_w, out_b, gamma_att, out):
     nc = tc.nc
-    by_partition = "b n (q hp) (wp i) c -> b q n (hp wp) i c"
-    xx_v = xx.rearrange(by_partition, q=PARTS, i=RUN)
-    xy_v = xy.rearrange(by_partition, q=PARTS, i=RUN)
+    by_partition = "b n (z hp) (wp i) c -> b z n (hp wp) i c"
+    xx_v = xx.rearrange(by_partition, z=PARTS, i=RUN)
+    xy_v = xy.rearrange(by_partition, z=PARTS, i=RUN)
     x_v = x.rearrange("b (m p) h w -> b m p (h w)", p=P)
     out_v = out.rearrange("b (m p) h w -> b m p (h w)", p=P)
 
     with ExitStack() as ctx:
         const = ctx.enter_context(tc.tile_pool(name="const", bufs=1))
-        stream = ctx.enter_context(tc.tile_pool(name="stream", bufs=B * PARTS))
-        xpool = ctx.enter_context(tc.tile_pool(name="xpool", bufs=OT))
-        respool = ctx.enter_context(tc.tile_pool(name="respool", bufs=6))
+        stream = ctx.enter_context(tc.tile_pool(name="stream", bufs=6))
+        xpool = ctx.enter_context(tc.tile_pool(name="xpool", bufs=6))
+        respool = ctx.enter_context(tc.tile_pool(name="respool", bufs=8))
         sums_pool = ctx.enter_context(tc.tile_pool(name="sums", bufs=2))
         big = ctx.enter_context(tc.tile_pool(name="big", bufs=2))
         junk = ctx.enter_context(tc.tile_pool(name="junk", bufs=1))
-        work = ctx.enter_context(tc.tile_pool(name="work", bufs=3))
+        work = ctx.enter_context(tc.tile_pool(name="work", bufs=2))
         psum = ctx.enter_context(tc.psum_pool(name="psum", bufs=8))
 
         ident = const.tile([P, P], F32)
         make_identity(nc, ident[:])
         ident_bf = const.tile([P, P], BF16)
         nc.vector.tensor_copy(out=ident_bf[:], in_=ident[:])
+
+        fold = const.tile([P, P // 2], BF16)
+        nc.vector.tensor_tensor(out=fold[:], in0=ident[:, 0::2], in1=ident[:, 1::2], op=ALU.add)
 
         one = const.tile([P, 1], F32)
         nc.vector.memset(one[:], 1.0)
@@ -63,14 +71,28 @@ def tile_axialattentionblock_pb_t_kernel(tc, xx, xy, x, norm2_w, out_w, out_b, g
 
         stream_of = {}
 
-        def load_part(b, q):
-            tiles = []
-            for name, view in (("xy", xy_v), ("xx", xx_v)):
-                t_sb = stream.tile([P, RUN, HD], BF16, tag=name, name="%s_%d_%d" % (name, b, q))
+        def load_half(b, z, h):
+            raw = stream.tile([P, 2 * NH * TILES * HEAD], BF16, tag="raw", name="raw%d%d%d" % (b, z, h))
+            stream_of[(b, z, h)] = raw
+            run = slice(h * TILES, (h + 1) * TILES)
+            if (b, z, h) in SUMMED:
+                raw_v = raw[:].rearrange("p (n r i c) -> p n r (i c)", n=NH, r=2, i=TILES)
                 for n in range(NH):
-                    nc.sync.dma_start(out=t_sb[:, :, n * HEAD : (n + 1) * HEAD], in_=view[b, q, n])
-                tiles.append(t_sb)
-            stream_of[(b, q)] = tiles
+                    for k, view in enumerate((xx_v, xy_v)):
+                        rows = view[b, z, n].rearrange("(q r) i c -> q r (i c)", r=2)
+                        nc.sync.dma_start(
+                            out=raw_v[k::2, n], in_=rows[:, :, h * TILES * HEAD : (h + 1) * TILES * HEAD]
+                        )
+            elif b == 0:
+                raw_v = raw[:].rearrange("p (k n i c) -> p k n i c", k=2, n=NH, i=TILES)
+                for k, view in enumerate((xy_v, xx_v)):
+                    for n in range(NH):
+                        nc.sync.dma_start(out=raw_v[:, k, n], in_=view[b, z, n][:, run])
+            else:
+                raw_v = raw[:].rearrange("p (k i n c) -> p k i n c", k=2, i=TILES, n=NH)
+                for k, view in enumerate((xy_v, xx_v)):
+                    for n in range(NH):
+                        nc.sync.dma_start(out=raw_v[:, k, :, n], in_=view[b, z, n][:, run])
 
         x_of = {}
 
@@ -79,7 +101,7 @@ def tile_axialattentionblock_pb_t_kernel(tc, xx, xy, x, norm2_w, out_w, out_b, g
             nc.sync.dma_start(out=x_sb[:], in_=x_v[b, m])
             x_of[(b, m)] = x_sb
 
-        load_part(0, 0)
+        load_half(0, 0, 0)
         vec_rows = const.tile([P, P], BF16)
         nc.vector.memset(vec_rows[:], 0.0)
         nc.scalar.dma_start(out=vec_rows[0:OT, :], in_=out_b.rearrange("(n c) -> n c", c=P))
@@ -87,12 +109,16 @@ def tile_axialattentionblock_pb_t_kernel(tc, xx, xy, x, norm2_w, out_w, out_b, g
         norm_rows = const.tile([P, T], BF16)
         nc.scalar.dma_start(out=norm_rows[:], in_=norm2_w.rearrange("(p t) -> p t", t=T))
         w_rows = const.tile([P, OT, HD], BF16)
-        load_part(0, 1)
+        load_half(0, 0, 1)
+        load_half(0, 1, 0)
+        load_half(0, 1, 1)
         nc.sync.dma_start(out=w_rows[:], in_=out_w.rearrange("(m p) j -> p m j", p=P))
+        load_half(1, 0, 0)
+        load_half(1, 0, 1)
         for m in range(OT):
             load_x(0, m)
-        load_part(1, 0)
-        load_part(1, 1)
+        load_half(1, 1, 0)
+        load_half(1, 1, 1)
 
         vecs = const.tile([P, 2 * OT], F32)
         gamma = vecs[:, OT : 2 * OT]
@@ -110,20 +136,21 @@ def tile_axialattentionblock_pb_t_kernel(tc, xx, xy, x, norm2_w, out_w, out_b, g
         w_codes = const.tile([P, HD], U32, align_bytes=64)
         w_scales = const.tile([P, HD], U8, align_bytes=64)
 
-        def quantise_weights():
+        def transpose_weights(h):
             words = w_rows[:].rearrange("p m j -> p (m j)").bitcast(F32)
             grouped_words = w_grouped[:].rearrange("k o t -> k (o t)").bitcast(F32)
-            half = HD // T * 2
-            for h in range(2):
-                wT = psum.tile([P, 2, 2, P], F32, tag="bank")
-                for d in range(2):
-                    m = 2 * h + d
-                    for u in range(2):
-                        nc.tensor.transpose(wT[:, d, u, :], words[:, m * half + u : (m + 1) * half : 2], ident[:])
-                nc.vector.tensor_copy(
-                    out=grouped_words[:, h * 2 * half : (h + 1) * 2 * half].rearrange("k (d o u) -> k d o u", d=2, u=2),
-                    in_=wT[:].rearrange("k d u o -> k d o u"),
-                )
+            run = HD // 2
+            wT = psum.tile([P, 2, U, P], F32, tag="bank")
+            for d in range(2):
+                m = 2 * h + d
+                for u in range(U):
+                    nc.tensor.transpose(wT[:, d, u, :], words[:, m * run + u : (m + 1) * run : 2], ident[:])
+            nc.vector.tensor_copy(
+                out=grouped_words[:, h * HD : (h + 1) * HD].rearrange("k (d o u) -> k d o u", d=2, u=U),
+                in_=wT[:].rearrange("k d u o -> k d o u"),
+            )
+
+        def quantise_weights():
             nc.vector.quantize_mx(
                 out=w_codes[:].bitcast(FP8X4), scales=w_scales[:], in_=w_grouped[:].rearrange("k o t -> k (o t)")
             )
@@ -134,42 +161,91 @@ def tile_axialattentionblock_pb_t_kernel(tc, xx, xy, x, norm2_w, out_w, out_b, g
         r_of = {}
         res_of = {}
         scaled_of = {}
+        grouped_of = {}
         codes_of = {}
+        acc_of = {}
+        words_of = {}
+        banks_of = {}
+        xyT_of = {}
 
-        def sum_unit(b, g, u):
+        def arrange_unit(b, z, h, u):
+            if u == 0:
+                words_of[(b, z, h)] = work.tile([P, U, 2, TILES, P], F32, tag="words", name="words%d%d%d" % (b, z, h))
+            raw = stream_of[(b, z, h)][:].bitcast(F32)
+            if (b, z, h) in SUMMED:
+                raw = raw.rearrange("p (n k i m u) -> p u k i n m", n=NH, k=2, i=TILES, u=U)
+            else:
+                raw = raw.rearrange("p (k n i m u) -> p u k i n m", n=NH, k=2, i=TILES, u=U)
+            for k in range(2):
+                nc.vector.tensor_copy(
+                    out=words_of[(b, z, h)][:, u, k].rearrange("p i (n m) -> p i n m", n=NH), in_=raw[:, u, k]
+                )
+
+        def transpose_unit(b, z, h, u):
+            banks = []
+            for k in range(2):
+                bank = psum.tile([P, TILES, P], F32, tag="bank", name="s%d_%d_%d_%d_%d" % (k, b, z, h, u))
+                for i in range(TILES):
+                    if (b, z, h) in SUMMED:
+                        for r in range(2):
+                            pairs = words_of[(b, z, h)][:, u, r, i, :].bitcast(BF16)
+                            nc.tensor.matmul(
+                                bank[:, i, r::2], lhsT=pairs[:, k::2], rhs=fold[:], start=True, stop=True
+                            )
+                        continue
+                    if b == 0:
+                        in_ = words_of[(b, z, h)][:, u, k, i, :]
+                    else:
+                        words = stream_of[(b, z, h)][:].bitcast(F32)
+                        first = (k * TILES + i) * (HD // 2)
+                        in_ = words[:, first + u : first + HD // 2 : 2]
+                    nc.tensor.transpose(bank[:, i, :], in_, ident[:])
+                banks.append(bank)
+            banks_of[(b, z, h, u)] = banks
+
+        def copy_unit(b, z, h, u):
+            if (b, z, h) in SUMMED:
+                return
+            xyT_sb = work.tile([P, CHUNK], F32, tag="xyT_sb", bufs=3)
+            nc.scalar.copy(out=xyT_sb[:], in_=banks_of[(b, z, h, u)][0][:].rearrange("c i p -> c (i p)"))
+            xyT_of[(b, z, h, u)] = xyT_sb
+
+        def add_unit(b, z, h, u):
+            g = z * CPP + h
             if g == 0 and u == 0:
                 sT_of[b] = big.tile([P, T, POS], F32, tag="sT", name="sT%d" % b)
                 sums_of[b] = (
                     sums_pool.tile([P, T, CHUNKS], F32, tag="sums", name="sums%d" % b),
                     sums_pool.tile([P, T, CHUNKS], F32, tag="sumsq", name="sumsq%d" % b),
                 )
-            q, h = divmod(g, CPP)
-            xy_sb, xx_sb = stream_of[(b, q)]
-            banks = []
-            for name, t_sb in (("xyT", xy_sb), ("xxT", xx_sb)):
-                words = t_sb[:].rearrange("p i j -> p (i j)").bitcast(F32)
-                bank = psum.tile([P, TILES, P], F32, tag="bank", name="%s_%d_%d_%d" % (name, b, g, u))
-                for i in range(TILES):
-                    first = (h * TILES + i) * (HD // 2)
-                    nc.tensor.transpose(bank[:, i, :], words[:, first + u : first + HD // 2 : 2], ident[:])
-                banks.append(bank)
-            xyT_sb = work.tile([P, CHUNK], F32, tag="xyT_sb")
-            nc.scalar.copy(out=xyT_sb[:], in_=banks[0][:].rearrange("c i p -> c (i p)"))
-            xy_pairs = xyT_sb[:].bitcast(BF16).rearrange("c (w e) -> c e w", e=2)
-            xx_pairs = banks[1][:].rearrange("c i p -> c (i p)").bitcast(BF16).rearrange("c (w e) -> c e w", e=2)
+            banks = banks_of[(b, z, h, u)]
             for e in range(2):
                 t = 2 * u + e
+                dst = sT_of[b][:, t, g * CHUNK : (g + 1) * CHUNK]
+                total = sums_of[b][0][:, t, g : g + 1]
+                if (b, z, h) in SUMMED:
+                    src = banks[e][:].rearrange("c i p -> c (i p)")
+                    if LEAVERS[t] == "S":
+                        nc.scalar.activation(out=dst, in_=src, func=ACT.Identity, accum_out=total)
+                    else:
+                        nc.vector.tensor_scalar(
+                            out=dst, in0=src, scalar1=1.0, scalar2=0.0, op0=ALU.mult, op1=ALU.add, accum_out=total
+                        )
+                    continue
+                xy_pairs = xyT_of[(b, z, h, u)][:].bitcast(BF16).rearrange("c (w e) -> c e w", e=2)
+                xx_pairs = banks[1][:].rearrange("c i p -> c (i p)").bitcast(BF16).rearrange("c (w e) -> c e w", e=2)
                 nc.vector.scalar_tensor_tensor(
-                    out=sT_of[b][:, t, g * CHUNK : (g + 1) * CHUNK],
+                    out=dst,
                     in0=xx_pairs[:, e, :],
                     scalar=1.0,
                     in1=xy_pairs[:, e, :],
                     op0=ALU.mult,
                     op1=ALU.add,
-                    accum_out=sums_of[b][0][:, t, g : g + 1],
+                    accum_out=total,
                 )
 
-        def square_unit(b, g, u):
+        def square_unit(b, z, h, u):
+            g = z * CPP + h
             for e in range(2):
                 t = 2 * u + e
                 squares = junk.tile([P, CHUNK], BF16, tag="squares")
@@ -184,12 +260,12 @@ def tile_axialattentionblock_pb_t_kernel(tc, xx, xy, x, norm2_w, out_w, out_b, g
             sums, sumsq = sums_of[b]
             sum_s = sums_pool.tile([P, T], F32, tag="sum_s")
             nc.vector.tensor_reduce(out=sum_s[:], in_=sums[:], axis=AX.X, op=ALU.add)
-            sum_q = sums_pool.tile([P, T], F32, tag="sum_q")
-            nc.vector.tensor_reduce(out=sum_q[:], in_=sumsq[:], axis=AX.X, op=ALU.add)
             sum_s2 = sums_pool.tile([P, T], F32, tag="sum_s2")
             nc.vector.scalar_tensor_tensor(
                 out=sum_s2[:], in0=sum_s[:], scalar=-1.0 / POS, in1=sum_s[:], op0=ALU.mult, op1=ALU.mult
             )
+            sum_q = sums_pool.tile([P, T], F32, tag="sum_q")
+            nc.vector.tensor_reduce(out=sum_q[:], in_=sumsq[:], axis=AX.X, op=ALU.add)
             centred = sums_pool.tile([P, T], F32, tag="centred")
             nc.vector.tensor_tensor(out=centred[:], in0=sum_s2[:], in1=sum_q[:], op=ALU.add)
             var = sums_pool.tile([P, T], F32, tag="var")
@@ -209,49 +285,54 @@ def tile_axialattentionblock_pb_t_kernel(tc, xx, xy, x, norm2_w, out_w, out_b, g
             nc.vector.tensor_tensor(out=r[:], in0=inv[:], in1=half_w[:], op=ALU.mult)
             r_of[b] = r
 
-        def residual_part(b, q, m):
-            res = respool.tile([P, PART], F32, tag="res", name="res%d%d%d" % (b, q, m))
+        def residual_part(b, z, m):
+            res = respool.tile([P, PART], F32, tag="res", name="res%d%d%d" % (b, z, m))
             nc.gpsimd.tensor_scalar(
                 out=res[:],
-                in0=x_of[(b, m)][:, q * PART : (q + 1) * PART],
+                in0=x_of[(b, m)][:, z * PART : (z + 1) * PART],
                 scalar1=1.0,
                 scalar2=bias_gamma[:, m : m + 1],
                 op0=ALU.mult,
                 op1=ALU.add,
             )
-            res_of[(b, q, m)] = res
+            res_of[(b, z, m)] = res
 
         def scale_chunk(b, g):
             scaled = work.tile([P, T, CHUNK], BF16, tag="scaled")
             for t in range(T):
                 part = sT_of[b][:, t, g * CHUNK : (g + 1) * CHUNK]
-                if t % 2 == 0:
-                    nc.scalar.activation(out=scaled[:, t, :], in_=part, func=ACT.Copy, scale=r_of[b][:, t : t + 1])
+                r = r_of[b][:, t : t + 1]
+                if SCALERS[b][g * T + t] == "S":
+                    nc.scalar.activation(out=scaled[:, t, :], in_=part, func=ACT.Copy, scale=r)
                 else:
                     nc.gpsimd.tensor_scalar(
-                        out=scaled[:, t, :], in0=part, scalar1=r_of[b][:, t : t + 1], scalar2=0.0, op0=ALU.mult, op1=ALU.add
+                        out=scaled[:, t, :], in0=part, scalar1=r, scalar2=0.0, op0=ALU.mult, op1=ALU.add
                     )
             scaled_of[(b, g)] = scaled
 
-        def quantise_chunk(b, g):
+        def group_chunk(b, g):
             grouped = work.tile([P, CHUNK, T], BF16, tag="grouped", align_bytes=64)
-            nc.vector.tensor_copy(
-                out=grouped[:].rearrange("c (q i) t -> c q t i", i=4),
-                in_=scaled_of[(b, g)][:].rearrange("c t (q i) -> c q t i", i=4),
-            )
+            dst = grouped[:].rearrange("c (q i) t -> c q t i", i=4)
+            src = scaled_of[(b, g)][:].rearrange("c t (q i) -> c q t i", i=4)
+            if GROUPERS[b][g] == "V":
+                nc.vector.tensor_copy(out=dst, in_=src)
+            else:
+                nc.scalar.copy(out=dst, in_=src)
+            grouped_of[(b, g)] = grouped
+
+        def quantise_chunk(b, g):
             g_codes = work.tile([P, CHUNK], U32, tag="g_codes", align_bytes=64)
             g_scales = work.tile([P, CHUNK], U8, tag="g_scales", align_bytes=64)
             nc.vector.quantize_mx(
-                out=g_codes[:].bitcast(FP8X4), scales=g_scales[:], in_=grouped[:].rearrange("c p t -> c (p t)")
+                out=g_codes[:].bitcast(FP8X4), scales=g_scales[:], in_=grouped_of[(b, g)][:].rearrange("c p t -> c (p t)")
             )
             codes_of[(b, g)] = (g_codes, g_scales)
 
-        def finish_chunk(b, g):
-            q, h = divmod(g, CPP)
+        def project_chunk(b, g):
             g_codes, g_scales = codes_of[(b, g)]
-            acc_of = {}
+            acc_of[(b, g)] = []
             for m in range(OT):
-                acc = psum.tile([P, CHUNK], F32, tag="bank")
+                acc = psum.tile([P, CHUNK], F32, tag="bank", name="acc%d_%d_%d" % (b, g, m))
                 nc.tensor.matmul_mx(
                     out=acc[:],
                     lhsT=w_codes[:, m * P : (m + 1) * P].bitcast(FP8X4),
@@ -261,47 +342,68 @@ def tile_axialattentionblock_pb_t_kernel(tc, xx, xy, x, norm2_w, out_w, out_b, g
                     start=True,
                     stop=True,
                 )
-                acc_of[m] = acc
+                acc_of[(b, g)].append(acc)
+
+        def finish_chunk(b, g):
+            z, h = divmod(g, CPP)
             for m in range(OT):
-                res = res_of[(b, q, m)][:].rearrange("o (p r) -> o p r", r=RUN)[:, :, h * TILES : (h + 1) * TILES]
+                res = res_of[(b, z, m)][:].rearrange("o (p r) -> o p r", r=RUN)[:, :, h * TILES : (h + 1) * TILES]
                 nc.vector.scalar_tensor_tensor(
                     out=res,
-                    in0=acc_of[m][:].rearrange("o (i p) -> o p i", i=TILES),
+                    in0=acc_of[(b, g)][m][:].rearrange("o (i p) -> o p i", i=TILES),
                     scalar=gamma[:, m : m + 1],
                     in1=res,
                     op0=ALU.mult,
                     op1=ALU.add,
                 )
                 if h == CPP - 1:
-                    nc.sync.dma_start(out=out_v[b, m][:, q * PART : (q + 1) * PART], in_=res_of[(b, q, m)][:])
+                    nc.sync.dma_start(out=out_v[b, m][:, z * PART : (z + 1) * PART], in_=res_of[(b, z, m)][:])
 
-        units = [(b, g, u) for b in range(B) for g in range(CHUNKS) for u in range(2)]
-        per_batch = CHUNKS * 2
-        for s in range(len(units) + 2 * CHUNKS + 4):
-            if s < len(units):
-                sum_unit(*units[s])
-            if s == 1:
-                prepare_vectors()
-            if s == 3:
-                quantise_weights()
-            if 0 < s <= len(units):
-                square_unit(*units[s - 1])
-            for b in range(B):
-                k = s - per_batch * (b + 1)
-                if k == 0:
-                    deviation(b)
-                if k == 1:
-                    scale_factors(b)
-                if k >= 1 and (k - 1) % 2 == 0 and (k - 1) // 2 < CHUNKS:
-                    c = (k - 1) // 2
-                    scale_chunk(b, c)
-                    if c % CPP == 0:
-                        for m in range(OT):
-                            residual_part(b, c // CPP, m)
-                if k >= 2 and (k - 2) % 2 == 0 and (k - 2) // 2 < CHUNKS:
-                    quantise_chunk(b, (k - 2) // 2)
-                if k >= 3 and (k - 3) % 2 == 0 and (k - 3) // 2 < CHUNKS:
-                    finish_chunk(b, (k - 3) // 2)
-                    if b == 0 and (k - 3) // 2 == CHUNKS - 1:
-                        for m in range(OT):
-                            load_x(1, m)
+        units = [(b, z, h, u) for b in range(B) for z in range(PARTS) for h in range(CPP) for u in range(U)]
+        per_batch = PARTS * CPP * U
+        engines = {
+            mybir.EngineType.PE,
+            mybir.EngineType.Activation,
+            mybir.EngineType.DVE,
+            mybir.EngineType.Pool,
+        }
+
+        plan = []
+
+        def at(step, work_item, *args):
+            plan.append((step, len(plan), work_item, args))
+
+        n = per_batch
+        step_of = [s for s in range(n)] + [n + 0.5 + 1 * k for k in range(n)]
+        for s in range(2 * n):
+            if s < n:
+                at(step_of[s] - 2, arrange_unit, *units[s])
+            at(step_of[s] - 1, transpose_unit, *units[s])
+            at(step_of[s], copy_unit, *units[s])
+            at(step_of[s] + 1, add_unit, *units[s])
+            at(step_of[s] + 1.75, square_unit, *units[s])
+        at(1, prepare_vectors)
+        for h in range(2):
+            at(5 + 4 * h, transpose_weights, h)
+        at(11, quantise_weights)
+        start = [13, 21.5]
+        period = [2, 2]
+        for b in range(B):
+            done = step_of[n * (b + 1) - 1] + 1.75
+            at(done + 1.5, deviation, b)
+            at(done + 2, scale_factors, b)
+            for g in range(CHUNKS):
+                x = start[b] + period[b] * g
+                at(x - 1.5, scale_chunk, b, g)
+                at(x, group_chunk, b, g)
+                at(x + 2, quantise_chunk, b, g)
+                at(x + 2.5, project_chunk, b, g)
+                at(x + 2.5, finish_chunk, b, g)
+            for z in range(PARTS):
+                for m in range(OT):
+                    at([8, 17][b] + 1.5 * (OT * z + m), residual_part, b, z, m)
+        for m in range(OT):
+            at(14, load_x, 1, m)
+        with tc.manual_schedule(engines=engines):
+            for step, number, work_item, args in sorted(plan, key=lambda entry: entry[:2]):
+                work_item(*args)

@@ -29,10 +29,10 @@ CPP = PART // CHUNK
 TILES = CHUNK // P
 OT = HD // P
 EPS = 1e-8
-SCALERS = ("GGGGGGGGGGGGGGGG", "GGSGGGSGGGSGGGSG")
-GROUPERS = ("SSSS", "SSSS")
+MIXERS = ("SSSV", "SSSS")
+RESIDUALS = "SSSS"
 SUMMED = ((0, 0, 0), (0, 0, 1), (0, 1, 0))
-LEAVERS = "VSVV"
+LEAVERS = "VVVS"
 
 FLOPS = 2 * B * HD * HD * POS
 
@@ -48,7 +48,7 @@ def tile_axialattentionblock_pb_t_kernel(tc, xx, xy, x, norm2_w, out_w, out_b, g
     with ExitStack() as ctx:
         const = ctx.enter_context(tc.tile_pool(name="const", bufs=1))
         stream = ctx.enter_context(tc.tile_pool(name="stream", bufs=6))
-        xpool = ctx.enter_context(tc.tile_pool(name="xpool", bufs=6))
+        xpool = ctx.enter_context(tc.tile_pool(name="xpool", bufs=3 * OT))
         respool = ctx.enter_context(tc.tile_pool(name="respool", bufs=8))
         sums_pool = ctx.enter_context(tc.tile_pool(name="sums", bufs=2))
         big = ctx.enter_context(tc.tile_pool(name="big", bufs=2))
@@ -96,10 +96,11 @@ def tile_axialattentionblock_pb_t_kernel(tc, xx, xy, x, norm2_w, out_w, out_b, g
 
         x_of = {}
 
-        def load_x(b, m):
-            x_sb = xpool.tile([P, POS], BF16, tag="x", name="x_%d_%d" % (b, m))
-            nc.sync.dma_start(out=x_sb[:], in_=x_v[b, m])
-            x_of[(b, m)] = x_sb
+        def load_x(b, z):
+            for m in range(OT):
+                x_sb = xpool.tile([P, PART], BF16, tag="x", name="x_%d_%d_%d" % (b, z, m))
+                nc.sync.dma_start(out=x_sb[:], in_=x_v[b, m][:, z * PART : (z + 1) * PART])
+                x_of[(b, z, m)] = x_sb
 
         load_half(0, 0, 0)
         vec_rows = const.tile([P, P], BF16)
@@ -114,11 +115,12 @@ def tile_axialattentionblock_pb_t_kernel(tc, xx, xy, x, norm2_w, out_w, out_b, g
         load_half(0, 1, 1)
         nc.sync.dma_start(out=w_rows[:], in_=out_w.rearrange("(m p) j -> p m j", p=P))
         load_half(1, 0, 0)
+        load_x(0, 0)
         load_half(1, 0, 1)
-        for m in range(OT):
-            load_x(0, m)
         load_half(1, 1, 0)
+        load_x(0, 1)
         load_half(1, 1, 1)
+        load_x(1, 0)
 
         vecs = const.tile([P, 2 * OT], F32)
         gamma = vecs[:, OT : 2 * OT]
@@ -287,37 +289,39 @@ def tile_axialattentionblock_pb_t_kernel(tc, xx, xy, x, norm2_w, out_w, out_b, g
 
         def residual_part(b, z, m):
             res = respool.tile([P, PART], F32, tag="res", name="res%d%d%d" % (b, z, m))
-            nc.gpsimd.tensor_scalar(
-                out=res[:],
-                in0=x_of[(b, m)][:, z * PART : (z + 1) * PART],
-                scalar1=1.0,
-                scalar2=bias_gamma[:, m : m + 1],
-                op0=ALU.mult,
-                op1=ALU.add,
-            )
+            x_part = x_of[(b, z, m)][:]
+            bias = bias_gamma[:, m : m + 1]
+            if RESIDUALS[m] == "S":
+                nc.scalar.activation(out=res[:], in_=x_part, func=ACT.Identity, bias=bias)
+            else:
+                nc.vector.tensor_scalar_add(out=res[:], in0=x_part, scalar1=bias)
             res_of[(b, z, m)] = res
 
         def scale_chunk(b, g):
+            part = sT_of[b][:, :, g * CHUNK : (g + 1) * CHUNK]
+            if MIXERS[b][g] == "V":
+                grouped = work.tile([P, CHUNK, T], BF16, tag="grouped", align_bytes=64, name="grouped%d%d" % (b, g))
+                nc.vector.tensor_tensor(
+                    out=grouped[:],
+                    in0=part.rearrange("c t p -> c p t"),
+                    in1=r_of[b][:].unsqueeze(1).to_broadcast([P, CHUNK, T]),
+                    op=ALU.mult,
+                )
+                grouped_of[(b, g)] = grouped
+                return
             scaled = work.tile([P, T, CHUNK], BF16, tag="scaled")
             for t in range(T):
-                part = sT_of[b][:, t, g * CHUNK : (g + 1) * CHUNK]
-                r = r_of[b][:, t : t + 1]
-                if SCALERS[b][g * T + t] == "S":
-                    nc.scalar.activation(out=scaled[:, t, :], in_=part, func=ACT.Copy, scale=r)
-                else:
-                    nc.gpsimd.tensor_scalar(
-                        out=scaled[:, t, :], in0=part, scalar1=r, scalar2=0.0, op0=ALU.mult, op1=ALU.add
-                    )
+                nc.vector.tensor_scalar_mul(out=scaled[:, t, :], in0=part[:, t, :], scalar1=r_of[b][:, t : t + 1])
             scaled_of[(b, g)] = scaled
 
         def group_chunk(b, g):
-            grouped = work.tile([P, CHUNK, T], BF16, tag="grouped", align_bytes=64)
-            dst = grouped[:].rearrange("c (q i) t -> c q t i", i=4)
-            src = scaled_of[(b, g)][:].rearrange("c t (q i) -> c q t i", i=4)
-            if GROUPERS[b][g] == "V":
-                nc.vector.tensor_copy(out=dst, in_=src)
-            else:
-                nc.scalar.copy(out=dst, in_=src)
+            if MIXERS[b][g] == "V":
+                return
+            grouped = work.tile([P, CHUNK, T], BF16, tag="grouped", align_bytes=64, name="grouped%d%d" % (b, g))
+            nc.scalar.copy(
+                out=grouped[:].rearrange("c (q i) t -> c q t i", i=4),
+                in_=scaled_of[(b, g)][:].rearrange("c t (q i) -> c q t i", i=4),
+            )
             grouped_of[(b, g)] = grouped
 
         def quantise_chunk(b, g):
@@ -374,7 +378,7 @@ def tile_axialattentionblock_pb_t_kernel(tc, xx, xy, x, norm2_w, out_w, out_b, g
             plan.append((step, len(plan), work_item, args))
 
         n = per_batch
-        step_of = [s for s in range(n)] + [n + 0.5 + 1 * k for k in range(n)]
+        step_of = [s for s in range(n)] + [n + 0.5 + 1.2 * k for k in range(n)]
         for s in range(2 * n):
             if s < n:
                 at(step_of[s] - 2, arrange_unit, *units[s])
@@ -382,28 +386,27 @@ def tile_axialattentionblock_pb_t_kernel(tc, xx, xy, x, norm2_w, out_w, out_b, g
             at(step_of[s], copy_unit, *units[s])
             at(step_of[s] + 1, add_unit, *units[s])
             at(step_of[s] + 1.75, square_unit, *units[s])
-        at(1, prepare_vectors)
+        at(-1, prepare_vectors)
         for h in range(2):
-            at(5 + 4 * h, transpose_weights, h)
-        at(11, quantise_weights)
-        start = [13, 21.5]
-        period = [2, 2]
+            at(5 + 2 * h, transpose_weights, h)
+        at(8.5, quantise_weights)
+        start = [12, 22]
+        period = [2.5, 1.5]
         for b in range(B):
             done = step_of[n * (b + 1) - 1] + 1.75
-            at(done + 1.5, deviation, b)
-            at(done + 2, scale_factors, b)
+            at(done + 1.25, deviation, b)
+            at(done + 2.5, scale_factors, b)
             for g in range(CHUNKS):
                 x = start[b] + period[b] * g
-                at(x - 1.5, scale_chunk, b, g)
+                at(x - 0.75, scale_chunk, b, g)
                 at(x, group_chunk, b, g)
-                at(x + 2, quantise_chunk, b, g)
-                at(x + 2.5, project_chunk, b, g)
+                at(x + 1.25, quantise_chunk, b, g)
+                at(x + 2, project_chunk, b, g)
                 at(x + 2.5, finish_chunk, b, g)
             for z in range(PARTS):
                 for m in range(OT):
-                    at([8, 17][b] + 1.5 * (OT * z + m), residual_part, b, z, m)
-        for m in range(OT):
-            at(14, load_x, 1, m)
+                    at([10, 18][b] + 1 * (OT * z + m), residual_part, b, z, m)
+        at(12, load_x, 1, 1)
         with tc.manual_schedule(engines=engines):
             for step, number, work_item, args in sorted(plan, key=lambda entry: entry[:2]):
                 work_item(*args)

@@ -28,11 +28,10 @@ CHUNKS = POS // CHUNK
 CPP = PART // CHUNK
 TILES = CHUNK // P
 OT = HD // P
+QUART = P // NH
 EPS = 1e-8
-MIXERS = ("SSSV", "SSSS")
+MIXERS = ("VSVS", "VSVS")
 RESIDUALS = "SSSS"
-SUMMED = ((0, 0, 0), (0, 0, 1), (0, 1, 0))
-LEAVERS = "VVVS"
 
 FLOPS = 2 * B * HD * HD * POS
 
@@ -47,11 +46,11 @@ def tile_axialattentionblock_pb_t_kernel(tc, xx, xy, x, norm2_w, out_w, out_b, g
 
     with ExitStack() as ctx:
         const = ctx.enter_context(tc.tile_pool(name="const", bufs=1))
-        stream = ctx.enter_context(tc.tile_pool(name="stream", bufs=6))
+        stream = ctx.enter_context(tc.tile_pool(name="stream", bufs=3))
         xpool = ctx.enter_context(tc.tile_pool(name="xpool", bufs=3 * OT))
         respool = ctx.enter_context(tc.tile_pool(name="respool", bufs=8))
         sums_pool = ctx.enter_context(tc.tile_pool(name="sums", bufs=2))
-        big = ctx.enter_context(tc.tile_pool(name="big", bufs=2))
+        spool = ctx.enter_context(tc.tile_pool(name="spool", bufs=B * PARTS))
         junk = ctx.enter_context(tc.tile_pool(name="junk", bufs=1))
         work = ctx.enter_context(tc.tile_pool(name="work", bufs=2))
         psum = ctx.enter_context(tc.psum_pool(name="psum", bufs=8))
@@ -61,9 +60,6 @@ def tile_axialattentionblock_pb_t_kernel(tc, xx, xy, x, norm2_w, out_w, out_b, g
         ident_bf = const.tile([P, P], BF16)
         nc.vector.tensor_copy(out=ident_bf[:], in_=ident[:])
 
-        fold = const.tile([P, P // 2], BF16)
-        nc.vector.tensor_tensor(out=fold[:], in0=ident[:, 0::2], in1=ident[:, 1::2], op=ALU.add)
-
         one = const.tile([P, 1], F32)
         nc.vector.memset(one[:], 1.0)
         one_root = const.tile([P, 1], F32)
@@ -71,28 +67,16 @@ def tile_axialattentionblock_pb_t_kernel(tc, xx, xy, x, norm2_w, out_w, out_b, g
 
         stream_of = {}
 
-        def load_half(b, z, h):
-            raw = stream.tile([P, 2 * NH * TILES * HEAD], BF16, tag="raw", name="raw%d%d%d" % (b, z, h))
-            stream_of[(b, z, h)] = raw
-            run = slice(h * TILES, (h + 1) * TILES)
-            if (b, z, h) in SUMMED:
-                raw_v = raw[:].rearrange("p (n r i c) -> p n r (i c)", n=NH, r=2, i=TILES)
+        def load_part(b, z, pieces=1):
+            tiles = []
+            for name in ("xx", "xy"):
+                tiles.append(stream.tile([P, NH, RUN, HEAD], BF16, tag=name, name="%s_%d_%d" % (name, b, z)))
+            for k in range(pieces):
+                run = slice(k * RUN // pieces, (k + 1) * RUN // pieces)
                 for n in range(NH):
-                    for k, view in enumerate((xx_v, xy_v)):
-                        rows = view[b, z, n].rearrange("(q r) i c -> q r (i c)", r=2)
-                        nc.sync.dma_start(
-                            out=raw_v[k::2, n], in_=rows[:, :, h * TILES * HEAD : (h + 1) * TILES * HEAD]
-                        )
-            elif b == 0:
-                raw_v = raw[:].rearrange("p (k n i c) -> p k n i c", k=2, n=NH, i=TILES)
-                for k, view in enumerate((xy_v, xx_v)):
-                    for n in range(NH):
-                        nc.sync.dma_start(out=raw_v[:, k, n], in_=view[b, z, n][:, run])
-            else:
-                raw_v = raw[:].rearrange("p (k i n c) -> p k i n c", k=2, i=TILES, n=NH)
-                for k, view in enumerate((xy_v, xx_v)):
-                    for n in range(NH):
-                        nc.sync.dma_start(out=raw_v[:, k, :, n], in_=view[b, z, n][:, run])
+                    for t_sb, view in zip(tiles, (xx_v, xy_v)):
+                        nc.sync.dma_start(out=t_sb[:, n, run], in_=view[b, z, n][:, run])
+            stream_of[(b, z)] = tiles
 
         x_of = {}
 
@@ -102,7 +86,7 @@ def tile_axialattentionblock_pb_t_kernel(tc, xx, xy, x, norm2_w, out_w, out_b, g
                 nc.sync.dma_start(out=x_sb[:], in_=x_v[b, m][:, z * PART : (z + 1) * PART])
                 x_of[(b, z, m)] = x_sb
 
-        load_half(0, 0, 0)
+        load_part(0, 0, CPP)
         vec_rows = const.tile([P, P], BF16)
         nc.vector.memset(vec_rows[:], 0.0)
         nc.scalar.dma_start(out=vec_rows[0:OT, :], in_=out_b.rearrange("(n c) -> n c", c=P))
@@ -110,16 +94,12 @@ def tile_axialattentionblock_pb_t_kernel(tc, xx, xy, x, norm2_w, out_w, out_b, g
         norm_rows = const.tile([P, T], BF16)
         nc.scalar.dma_start(out=norm_rows[:], in_=norm2_w.rearrange("(p t) -> p t", t=T))
         w_rows = const.tile([P, OT, HD], BF16)
-        load_half(0, 0, 1)
-        load_half(0, 1, 0)
-        load_half(0, 1, 1)
+        load_part(0, 1)
         nc.sync.dma_start(out=w_rows[:], in_=out_w.rearrange("(m p) j -> p m j", p=P))
-        load_half(1, 0, 0)
+        load_part(1, 0)
         load_x(0, 0)
-        load_half(1, 0, 1)
-        load_half(1, 1, 0)
+        load_part(1, 1)
         load_x(0, 1)
-        load_half(1, 1, 1)
         load_x(1, 0)
 
         vecs = const.tile([P, 2 * OT], F32)
@@ -157,117 +137,88 @@ def tile_axialattentionblock_pb_t_kernel(tc, xx, xy, x, norm2_w, out_w, out_b, g
                 out=w_codes[:].bitcast(FP8X4), scales=w_scales[:], in_=w_grouped[:].rearrange("k o t -> k (o t)")
             )
 
-        sT_of = {}
-        sums_of = {}
+        s_of = {}
+        squares_of = {}
+        stat_banks = {}
+        partial_of = {}
         std_of = {}
         r_of = {}
         res_of = {}
+        tiles_of = {}
         scaled_of = {}
         grouped_of = {}
         codes_of = {}
         acc_of = {}
-        words_of = {}
-        banks_of = {}
-        xyT_of = {}
 
-        def arrange_unit(b, z, h, u):
-            if u == 0:
-                words_of[(b, z, h)] = work.tile([P, U, 2, TILES, P], F32, tag="words", name="words%d%d%d" % (b, z, h))
-            raw = stream_of[(b, z, h)][:].bitcast(F32)
-            if (b, z, h) in SUMMED:
-                raw = raw.rearrange("p (n k i m u) -> p u k i n m", n=NH, k=2, i=TILES, u=U)
-            else:
-                raw = raw.rearrange("p (k n i m u) -> p u k i n m", n=NH, k=2, i=TILES, u=U)
-            for k in range(2):
-                nc.vector.tensor_copy(
-                    out=words_of[(b, z, h)][:, u, k].rearrange("p i (n m) -> p i n m", n=NH), in_=raw[:, u, k]
+        def add_unit(b, z, h):
+            if h == 0:
+                s_of[(b, z)] = spool.tile([P, RUN, T, P], F32, tag="s", name="s%d%d" % (b, z))
+            run = slice(h * TILES, (h + 1) * TILES)
+            for n in range(NH):
+                xx_n, xy_n = (t_sb[:, n, run].rearrange("p i (m t) -> p i t m", t=T) for t_sb in stream_of[(b, z)])
+                nc.vector.tensor_tensor(
+                    out=s_of[(b, z)][:, run, :, n * QUART : (n + 1) * QUART], in0=xx_n, in1=xy_n, op=ALU.add
                 )
 
-        def transpose_unit(b, z, h, u):
-            banks = []
-            for k in range(2):
-                bank = psum.tile([P, TILES, P], F32, tag="bank", name="s%d_%d_%d_%d_%d" % (k, b, z, h, u))
+        def square_unit(b, z, h):
+            squares = work.tile([P, TILES, T, P], F32, tag="squares", bufs=2, name="squares%d%d%d" % (b, z, h))
+            nc.scalar.activation(
+                out=squares[:].rearrange("p i t m -> p (i t m)"),
+                in_=s_of[(b, z)][:, h * TILES : (h + 1) * TILES].rearrange("p i t m -> p (i t m)"),
+                func=ACT.Square,
+            )
+            squares_of[(b, z, h)] = squares
+
+        def turn(out, in_, start=True, stop=True):
+            nc.tensor.matmul(out, lhsT=in_, rhs=ident[:], is_transpose=True, start=start, stop=stop)
+
+        def gather(b, z, tiles, k):
+            bank = psum.tile([P, T, P], F32, tag="bank", name="stat%d%d%d%d" % (b, z, tiles.start, k))
+            for t in range(T):
+                for i in tiles:
+                    if k == 0:
+                        in_ = s_of[(b, z)][:, i, t]
+                    else:
+                        in_ = squares_of[(b, z, i // TILES)][:, i % TILES, t]
+                    turn(bank[:, t], in_, i == tiles.start, i == tiles.stop - 1)
+            stat_banks[(b, z, tiles.start, k)] = bank
+
+        def reduce(b, z, tiles, k):
+            spans = POS // (P * len(tiles))
+            slot = (z * RUN + tiles.start) // len(tiles)
+            bank = stat_banks[(b, z, tiles.start, k)]
+            if (b, k) not in partial_of:
+                partial_of[(b, k)] = sums_pool.tile([P, T, spans], F32, tag="partial%d" % k, name="partial%d%d" % (b, k))
+            partial = partial_of[(b, k)]
+            nc.vector.tensor_reduce(out=partial[:, :, slot], in_=bank[:], axis=AX.X, op=ALU.add)
+
+        def turn_half(z, h):
+            for t in range(T):
+                bank = psum.tile([P, TILES, P], F32, tag="bank", name="half%d%d%d" % (z, h, t))
                 for i in range(TILES):
-                    if (b, z, h) in SUMMED:
-                        for r in range(2):
-                            pairs = words_of[(b, z, h)][:, u, r, i, :].bitcast(BF16)
-                            nc.tensor.matmul(
-                                bank[:, i, r::2], lhsT=pairs[:, k::2], rhs=fold[:], start=True, stop=True
-                            )
-                        continue
-                    if b == 0:
-                        in_ = words_of[(b, z, h)][:, u, k, i, :]
-                    else:
-                        words = stream_of[(b, z, h)][:].bitcast(F32)
-                        first = (k * TILES + i) * (HD // 2)
-                        in_ = words[:, first + u : first + HD // 2 : 2]
-                    nc.tensor.transpose(bank[:, i, :], in_, ident[:])
-                banks.append(bank)
-            banks_of[(b, z, h, u)] = banks
+                    turn(bank[:, i], s_of[(0, z)][:, h * TILES + i, t])
+                stat_banks[(z, h, t)] = bank
 
-        def copy_unit(b, z, h, u):
-            if (b, z, h) in SUMMED:
-                return
-            xyT_sb = work.tile([P, CHUNK], F32, tag="xyT_sb", bufs=3)
-            nc.scalar.copy(out=xyT_sb[:], in_=banks_of[(b, z, h, u)][0][:].rearrange("c i p -> c (i p)"))
-            xyT_of[(b, z, h, u)] = xyT_sb
-
-        def add_unit(b, z, h, u):
-            g = z * CPP + h
-            if g == 0 and u == 0:
-                sT_of[b] = big.tile([P, T, POS], F32, tag="sT", name="sT%d" % b)
-                sums_of[b] = (
-                    sums_pool.tile([P, T, CHUNKS], F32, tag="sums", name="sums%d" % b),
-                    sums_pool.tile([P, T, CHUNKS], F32, tag="sumsq", name="sumsq%d" % b),
-                )
-            banks = banks_of[(b, z, h, u)]
-            for e in range(2):
-                t = 2 * u + e
-                dst = sT_of[b][:, t, g * CHUNK : (g + 1) * CHUNK]
-                total = sums_of[b][0][:, t, g : g + 1]
-                if (b, z, h) in SUMMED:
-                    src = banks[e][:].rearrange("c i p -> c (i p)")
-                    if LEAVERS[t] == "S":
-                        nc.scalar.activation(out=dst, in_=src, func=ACT.Identity, accum_out=total)
-                    else:
-                        nc.vector.tensor_scalar(
-                            out=dst, in0=src, scalar1=1.0, scalar2=0.0, op0=ALU.mult, op1=ALU.add, accum_out=total
-                        )
-                    continue
-                xy_pairs = xyT_of[(b, z, h, u)][:].bitcast(BF16).rearrange("c (w e) -> c e w", e=2)
-                xx_pairs = banks[1][:].rearrange("c i p -> c (i p)").bitcast(BF16).rearrange("c (w e) -> c e w", e=2)
-                nc.vector.scalar_tensor_tensor(
-                    out=dst,
-                    in0=xx_pairs[:, e, :],
-                    scalar=1.0,
-                    in1=xy_pairs[:, e, :],
-                    op0=ALU.mult,
-                    op1=ALU.add,
-                    accum_out=total,
-                )
-
-        def square_unit(b, z, h, u):
-            g = z * CPP + h
-            for e in range(2):
-                t = 2 * u + e
-                squares = junk.tile([P, CHUNK], BF16, tag="squares")
-                nc.scalar.activation(
-                    out=squares[:],
-                    in_=sT_of[b][:, t, g * CHUNK : (g + 1) * CHUNK],
-                    func=ACT.Square,
-                    accum_out=sums_of[b][1][:, t, g : g + 1],
-                )
+        def sum_half(z, h):
+            slot = z * CPP + h
+            for kind, t in ((1, 0), (0, 1), (1, 1), (0, 0), (1, 2), (0, 3), (1, 3), (0, 2)):
+                bank = stat_banks[(z, h, t)][:].rearrange("c i p -> c (i p)")
+                sums = partial_of[(0, kind)][:, t, slot : slot + 1]
+                if kind == 0:
+                    nc.vector.tensor_reduce(out=sums, in_=bank, axis=AX.X, op=ALU.add)
+                else:
+                    squares = junk.tile([P, CHUNK], BF16, tag="scrap_squares")
+                    nc.scalar.activation(out=squares[:], in_=bank, func=ACT.Square, accum_out=sums)
 
         def deviation(b):
-            sums, sumsq = sums_of[b]
             sum_s = sums_pool.tile([P, T], F32, tag="sum_s")
-            nc.vector.tensor_reduce(out=sum_s[:], in_=sums[:], axis=AX.X, op=ALU.add)
+            nc.vector.tensor_reduce(out=sum_s[:], in_=partial_of[(b, 0)][:], axis=AX.X, op=ALU.add)
+            sum_q = sums_pool.tile([P, T], F32, tag="sum_q")
+            nc.vector.tensor_reduce(out=sum_q[:], in_=partial_of[(b, 1)][:], axis=AX.X, op=ALU.add)
             sum_s2 = sums_pool.tile([P, T], F32, tag="sum_s2")
             nc.vector.scalar_tensor_tensor(
                 out=sum_s2[:], in0=sum_s[:], scalar=-1.0 / POS, in1=sum_s[:], op0=ALU.mult, op1=ALU.mult
             )
-            sum_q = sums_pool.tile([P, T], F32, tag="sum_q")
-            nc.vector.tensor_reduce(out=sum_q[:], in_=sumsq[:], axis=AX.X, op=ALU.add)
             centred = sums_pool.tile([P, T], F32, tag="centred")
             nc.vector.tensor_tensor(out=centred[:], in0=sum_s2[:], in1=sum_q[:], op=ALU.add)
             var = sums_pool.tile([P, T], F32, tag="var")
@@ -297,27 +248,43 @@ def tile_axialattentionblock_pb_t_kernel(tc, xx, xy, x, norm2_w, out_w, out_b, g
                 nc.vector.tensor_scalar_add(out=res[:], in0=x_part, scalar1=bias)
             res_of[(b, z, m)] = res
 
+        def turn_chunk(b, g):
+            z, h = divmod(g, CPP)
+            banks = []
+            for k in range(TILES):
+                bank = psum.tile([P, TILES, P], F32, tag="bank", name="turn%d%d%d" % (b, g, k))
+                for l in range(TILES):
+                    i, t = (k, l) if MIXERS[b][g] == "V" else (l, k)
+                    turn(bank[:, l], s_of[(b, z)][:, h * TILES + i, t])
+                banks.append(bank)
+            tiles_of[(b, g)] = banks
+
         def scale_chunk(b, g):
-            part = sT_of[b][:, :, g * CHUNK : (g + 1) * CHUNK]
             if MIXERS[b][g] == "V":
-                grouped = work.tile([P, CHUNK, T], BF16, tag="grouped", align_bytes=64, name="grouped%d%d" % (b, g))
-                nc.vector.tensor_tensor(
-                    out=grouped[:],
-                    in0=part.rearrange("c t p -> c p t"),
-                    in1=r_of[b][:].unsqueeze(1).to_broadcast([P, CHUNK, T]),
-                    op=ALU.mult,
-                )
+                grouped = work.tile([P, CHUNK, T], BF16, tag="grouped", bufs=3, align_bytes=64, name="grouped%d%d" % (b, g))
+                for i in range(TILES):
+                    nc.vector.tensor_tensor(
+                        out=grouped[:, i * P : (i + 1) * P],
+                        in0=tiles_of[(b, g)][i][:].rearrange("c t p -> c p t"),
+                        in1=r_of[b][:].unsqueeze(1).to_broadcast([P, P, T]),
+                        op=ALU.mult,
+                    )
                 grouped_of[(b, g)] = grouped
                 return
             scaled = work.tile([P, T, CHUNK], BF16, tag="scaled")
             for t in range(T):
-                nc.vector.tensor_scalar_mul(out=scaled[:, t, :], in0=part[:, t, :], scalar1=r_of[b][:, t : t + 1])
+                nc.scalar.activation(
+                    out=scaled[:, t],
+                    in_=tiles_of[(b, g)][t][:].rearrange("c i p -> c (i p)"),
+                    func=ACT.Copy,
+                    scale=r_of[b][:, t : t + 1],
+                )
             scaled_of[(b, g)] = scaled
 
         def group_chunk(b, g):
             if MIXERS[b][g] == "V":
                 return
-            grouped = work.tile([P, CHUNK, T], BF16, tag="grouped", align_bytes=64, name="grouped%d%d" % (b, g))
+            grouped = work.tile([P, CHUNK, T], BF16, tag="grouped", bufs=3, align_bytes=64, name="grouped%d%d" % (b, g))
             nc.scalar.copy(
                 out=grouped[:].rearrange("c (q i) t -> c q t i", i=4),
                 in_=scaled_of[(b, g)][:].rearrange("c t (q i) -> c q t i", i=4),
@@ -363,50 +330,85 @@ def tile_axialattentionblock_pb_t_kernel(tc, xx, xy, x, norm2_w, out_w, out_b, g
                 if h == CPP - 1:
                     nc.sync.dma_start(out=out_v[b, m][:, z * PART : (z + 1) * PART], in_=res_of[(b, z, m)][:])
 
-        units = [(b, z, h, u) for b in range(B) for z in range(PARTS) for h in range(CPP) for u in range(U)]
-        per_batch = PARTS * CPP * U
-        engines = {
-            mybir.EngineType.PE,
-            mybir.EngineType.Activation,
-            mybir.EngineType.DVE,
-            mybir.EngineType.Pool,
-        }
+        halves = [(z, h) for z in range(PARTS) for h in range(CPP)]
+        whole = range(RUN)
 
-        plan = []
+        def residuals(b, z, ms):
+            for m in ms:
+                residual_part(b, z, m)
 
-        def at(step, work_item, *args):
-            plan.append((step, len(plan), work_item, args))
-
-        n = per_batch
-        step_of = [s for s in range(n)] + [n + 0.5 + 1.2 * k for k in range(n)]
-        for s in range(2 * n):
-            if s < n:
-                at(step_of[s] - 2, arrange_unit, *units[s])
-            at(step_of[s] - 1, transpose_unit, *units[s])
-            at(step_of[s], copy_unit, *units[s])
-            at(step_of[s] + 1, add_unit, *units[s])
-            at(step_of[s] + 1.75, square_unit, *units[s])
-        at(-1, prepare_vectors)
+        first, second, third, fourth = halves
+        add_unit(0, *first)
+        prepare_vectors()
+        gather(0, 0, range(0, TILES), 0)
+        square_unit(0, *first)
+        add_unit(0, *second)
+        reduce(0, 0, range(0, TILES), 0)
+        gather(0, 0, range(TILES, RUN), 0)
+        gather(0, 0, range(0, TILES), 1)
+        square_unit(0, *second)
+        add_unit(0, *third)
+        reduce(0, 0, range(0, TILES), 1)
+        gather(0, 0, range(TILES, RUN), 1)
+        turn_half(*third)
+        add_unit(0, *fourth)
+        reduce(0, 0, range(TILES, RUN), 0)
+        reduce(0, 0, range(TILES, RUN), 1)
+        sum_half(*third)
+        turn_half(*fourth)
+        sum_half(*fourth)
+        deviation(0)
         for h in range(2):
-            at(5 + 2 * h, transpose_weights, h)
-        at(8.5, quantise_weights)
-        start = [12, 22]
-        period = [2.5, 1.5]
-        for b in range(B):
-            done = step_of[n * (b + 1) - 1] + 1.75
-            at(done + 1.25, deviation, b)
-            at(done + 2.5, scale_factors, b)
-            for g in range(CHUNKS):
-                x = start[b] + period[b] * g
-                at(x - 0.75, scale_chunk, b, g)
-                at(x, group_chunk, b, g)
-                at(x + 1.25, quantise_chunk, b, g)
-                at(x + 2, project_chunk, b, g)
-                at(x + 2.5, finish_chunk, b, g)
-            for z in range(PARTS):
-                for m in range(OT):
-                    at([10, 18][b] + 1 * (OT * z + m), residual_part, b, z, m)
-        at(12, load_x, 1, 1)
-        with tc.manual_schedule(engines=engines):
-            for step, number, work_item, args in sorted(plan, key=lambda entry: entry[:2]):
-                work_item(*args)
+            transpose_weights(h)
+        scale_factors(0)
+        add_unit(1, *first)
+        quantise_weights()
+        residuals(0, 0, (0, 1))
+        square_unit(1, *first)
+        residuals(0, 0, (2, 3))
+        turn_chunk(0, 0)
+        scale_chunk(0, 0)
+        group_chunk(0, 0)
+        for k, (z, h) in enumerate(halves):
+            if h == 1:
+                for kind in range(2):
+                    gather(1, z, whole, kind)
+            if k + 1 < CHUNKS:
+                add_unit(1, *halves[k + 1])
+            if k > 0:
+                finish_chunk(0, k - 1)
+            quantise_chunk(0, k)
+            if h == 1:
+                for kind in range(2):
+                    reduce(1, z, whole, kind)
+            if k + 1 < CHUNKS:
+                turn_chunk(0, k + 1)
+            project_chunk(0, k)
+            if k + 1 < CHUNKS:
+                scale_chunk(0, k + 1)
+                group_chunk(0, k + 1)
+                square_unit(1, *halves[k + 1])
+            if k in (0, 1):
+                residuals(0, 1, (2 * k, 2 * k + 1))
+            if k in (2, 3):
+                residuals(1, 0, (2 * k - 4, 2 * k - 3))
+            if k == 2:
+                load_x(1, 1)
+        deviation(1)
+        turn_chunk(1, 0)
+        finish_chunk(0, CHUNKS - 1)
+        scale_factors(1)
+        scale_chunk(1, 0)
+        group_chunk(1, 0)
+        for k, (z, h) in enumerate(halves):
+            if k > 0:
+                finish_chunk(1, k - 1)
+            if k + 1 < CHUNKS:
+                turn_chunk(1, k + 1)
+                scale_chunk(1, k + 1)
+                group_chunk(1, k + 1)
+            quantise_chunk(1, k)
+            project_chunk(1, k)
+            if k in (0, 1):
+                residuals(1, 1, (2 * k, 2 * k + 1))
+        finish_chunk(1, CHUNKS - 1)

@@ -53,7 +53,7 @@ def tile_axialattentionblock_pb_t_kernel(tc, xx, xy, x, norm2_w, out_w, out_b, g
         spool = ctx.enter_context(tc.tile_pool(name="spool", bufs=B * PARTS))
         junk = ctx.enter_context(tc.tile_pool(name="junk", bufs=1))
         work = ctx.enter_context(tc.tile_pool(name="work", bufs=2))
-        psum = ctx.enter_context(tc.psum_pool(name="psum", bufs=8))
+        psum = ctx.enter_context(tc.psum_pool(name="psum", bufs=6))
 
         ident = const.tile([P, P], F32)
         make_identity(nc, ident[:])
@@ -127,7 +127,7 @@ def tile_axialattentionblock_pb_t_kernel(tc, xx, xy, x, norm2_w, out_w, out_b, g
                 m = 2 * h + d
                 for u in range(U):
                     nc.tensor.transpose(wT[:, d, u, :], words[:, m * run + u : (m + 1) * run : 2], ident[:])
-            nc.vector.tensor_copy(
+            nc.scalar.copy(
                 out=grouped_words[:, h * HD : (h + 1) * HD].rearrange("k (d o u) -> k d o u", d=2, u=U),
                 in_=wT[:].rearrange("k d u o -> k d o u"),
             )
@@ -150,18 +150,18 @@ def tile_axialattentionblock_pb_t_kernel(tc, xx, xy, x, norm2_w, out_w, out_b, g
         codes_of = {}
         acc_of = {}
 
-        def add_unit(b, z, h):
-            if h == 0:
+        def add_unit(b, z, h, heads=range(NH)):
+            if (b, z) not in s_of:
                 s_of[(b, z)] = spool.tile([P, RUN, T, P], F32, tag="s", name="s%d%d" % (b, z))
             run = slice(h * TILES, (h + 1) * TILES)
-            for n in range(NH):
+            for n in heads:
                 xx_n, xy_n = (t_sb[:, n, run].rearrange("p i (m t) -> p i t m", t=T) for t_sb in stream_of[(b, z)])
                 nc.vector.tensor_tensor(
                     out=s_of[(b, z)][:, run, :, n * QUART : (n + 1) * QUART], in0=xx_n, in1=xy_n, op=ALU.add
                 )
 
         def square_unit(b, z, h):
-            squares = work.tile([P, TILES, T, P], F32, tag="squares", bufs=2, name="squares%d%d%d" % (b, z, h))
+            squares = work.tile([P, TILES, T, P], F32, tag="squares", bufs=3, name="squares%d%d%d" % (b, z, h))
             nc.scalar.activation(
                 out=squares[:].rearrange("p i t m -> p (i t m)"),
                 in_=s_of[(b, z)][:, h * TILES : (h + 1) * TILES].rearrange("p i t m -> p (i t m)"),
@@ -172,36 +172,37 @@ def tile_axialattentionblock_pb_t_kernel(tc, xx, xy, x, norm2_w, out_w, out_b, g
         def turn(out, in_, start=True, stop=True):
             nc.tensor.matmul(out, lhsT=in_, rhs=ident[:], is_transpose=True, start=start, stop=stop)
 
-        def gather(b, z, tiles, k):
-            bank = psum.tile([P, T, P], F32, tag="bank", name="stat%d%d%d%d" % (b, z, tiles.start, k))
-            for t in range(T):
+        def gather(b, z, tiles, k, slots=range(T)):
+            if (b, z, tiles.start, k) not in stat_banks:
+                stat_banks[(b, z, tiles.start, k)] = psum.tile(
+                    [P, T, P], F32, tag="stat", bufs=2, name="stat%d%d%d%d" % (b, z, tiles.start, k)
+                )
+            bank = stat_banks[(b, z, tiles.start, k)]
+            for t in slots:
                 for i in tiles:
                     if k == 0:
                         in_ = s_of[(b, z)][:, i, t]
                     else:
                         in_ = squares_of[(b, z, i // TILES)][:, i % TILES, t]
                     turn(bank[:, t], in_, i == tiles.start, i == tiles.stop - 1)
-            stat_banks[(b, z, tiles.start, k)] = bank
 
-        def reduce(b, z, tiles, k):
-            spans = POS // (P * len(tiles))
-            slot = (z * RUN + tiles.start) // len(tiles)
+        def reduce(b, z, tiles, k, slot):
             bank = stat_banks[(b, z, tiles.start, k)]
-            if (b, k) not in partial_of:
-                partial_of[(b, k)] = sums_pool.tile([P, T, spans], F32, tag="partial%d" % k, name="partial%d%d" % (b, k))
-            partial = partial_of[(b, k)]
-            nc.vector.tensor_reduce(out=partial[:, :, slot], in_=bank[:], axis=AX.X, op=ALU.add)
+            nc.vector.tensor_reduce(out=partial_of[(b, k)][:, :, slot], in_=bank[:], axis=AX.X, op=ALU.add)
 
-        def turn_half(z, h):
-            for t in range(T):
+        def open_sums(b, slots):
+            for k in range(2):
+                partial_of[(b, k)] = sums_pool.tile([P, T, slots], F32, tag="partial%d" % k, name="partial%d%d" % (b, k))
+
+        def turn_half(z, h, slots=range(T)):
+            for t in slots:
                 bank = psum.tile([P, TILES, P], F32, tag="bank", name="half%d%d%d" % (z, h, t))
                 for i in range(TILES):
                     turn(bank[:, i], s_of[(0, z)][:, h * TILES + i, t])
                 stat_banks[(z, h, t)] = bank
 
-        def sum_half(z, h):
-            slot = z * CPP + h
-            for kind, t in ((1, 0), (0, 1), (1, 1), (0, 0), (1, 2), (0, 3), (1, 3), (0, 2)):
+        def sum_half(z, h, kind, slot, slots=range(T)):
+            for t in slots:
                 bank = stat_banks[(z, h, t)][:].rearrange("c i p -> c (i p)")
                 sums = partial_of[(0, kind)][:, t, slot : slot + 1]
                 if kind == 0:
@@ -248,38 +249,41 @@ def tile_axialattentionblock_pb_t_kernel(tc, xx, xy, x, norm2_w, out_w, out_b, g
                 nc.vector.tensor_scalar_add(out=res[:], in0=x_part, scalar1=bias)
             res_of[(b, z, m)] = res
 
-        def turn_chunk(b, g):
+        def turn_chunk(b, g, ks=range(TILES)):
             z, h = divmod(g, CPP)
-            banks = []
-            for k in range(TILES):
+            banks = tiles_of.setdefault((b, g), {})
+            for k in ks:
                 bank = psum.tile([P, TILES, P], F32, tag="bank", name="turn%d%d%d" % (b, g, k))
                 for l in range(TILES):
                     i, t = (k, l) if MIXERS[b][g] == "V" else (l, k)
                     turn(bank[:, l], s_of[(b, z)][:, h * TILES + i, t])
-                banks.append(bank)
-            tiles_of[(b, g)] = banks
+                banks[k] = bank
 
-        def scale_chunk(b, g):
+        def scale_chunk(b, g, ks=range(TILES)):
             if MIXERS[b][g] == "V":
-                grouped = work.tile([P, CHUNK, T], BF16, tag="grouped", bufs=3, align_bytes=64, name="grouped%d%d" % (b, g))
-                for i in range(TILES):
+                if (b, g) not in grouped_of:
+                    grouped_of[(b, g)] = work.tile(
+                        [P, CHUNK, T], BF16, tag="grouped", bufs=3, align_bytes=64, name="grouped%d%d" % (b, g)
+                    )
+                grouped = grouped_of[(b, g)]
+                for i in ks:
                     nc.vector.tensor_tensor(
                         out=grouped[:, i * P : (i + 1) * P],
                         in0=tiles_of[(b, g)][i][:].rearrange("c t p -> c p t"),
                         in1=r_of[b][:].unsqueeze(1).to_broadcast([P, P, T]),
                         op=ALU.mult,
                     )
-                grouped_of[(b, g)] = grouped
                 return
-            scaled = work.tile([P, T, CHUNK], BF16, tag="scaled")
-            for t in range(T):
+            if (b, g) not in scaled_of:
+                scaled_of[(b, g)] = work.tile([P, T, CHUNK], BF16, tag="scaled", name="scaled%d%d" % (b, g))
+            scaled = scaled_of[(b, g)]
+            for t in ks:
                 nc.scalar.activation(
                     out=scaled[:, t],
                     in_=tiles_of[(b, g)][t][:].rearrange("c i p -> c (i p)"),
                     func=ACT.Copy,
                     scale=r_of[b][:, t : t + 1],
                 )
-            scaled_of[(b, g)] = scaled
 
         def group_chunk(b, g):
             if MIXERS[b][g] == "V":
@@ -299,10 +303,10 @@ def tile_axialattentionblock_pb_t_kernel(tc, xx, xy, x, norm2_w, out_w, out_b, g
             )
             codes_of[(b, g)] = (g_codes, g_scales)
 
-        def project_chunk(b, g):
+        def project_chunk(b, g, ms=range(OT)):
             g_codes, g_scales = codes_of[(b, g)]
-            acc_of[(b, g)] = []
-            for m in range(OT):
+            accs = acc_of.setdefault((b, g), {})
+            for m in ms:
                 acc = psum.tile([P, CHUNK], F32, tag="bank", name="acc%d_%d_%d" % (b, g, m))
                 nc.tensor.matmul_mx(
                     out=acc[:],
@@ -313,11 +317,11 @@ def tile_axialattentionblock_pb_t_kernel(tc, xx, xy, x, norm2_w, out_w, out_b, g
                     start=True,
                     stop=True,
                 )
-                acc_of[(b, g)].append(acc)
+                accs[m] = acc
 
-        def finish_chunk(b, g):
+        def finish_chunk(b, g, ms=range(OT)):
             z, h = divmod(g, CPP)
-            for m in range(OT):
+            for m in ms:
                 res = res_of[(b, z, m)][:].rearrange("o (p r) -> o p r", r=RUN)[:, :, h * TILES : (h + 1) * TILES]
                 nc.vector.scalar_tensor_tensor(
                     out=res,
@@ -329,86 +333,101 @@ def tile_axialattentionblock_pb_t_kernel(tc, xx, xy, x, norm2_w, out_w, out_b, g
                 )
                 if h == CPP - 1:
                     nc.sync.dma_start(out=out_v[b, m][:, z * PART : (z + 1) * PART], in_=res_of[(b, z, m)][:])
+        whole, low = range(RUN), range(TILES)
+        engines = {mybir.EngineType.PE, mybir.EngineType.Activation, mybir.EngineType.DVE, mybir.EngineType.Pool}
 
-        halves = [(z, h) for z in range(PARTS) for h in range(CPP)]
-        whole = range(RUN)
-
-        def residuals(b, z, ms):
+        def residuals(b, z, ms=range(OT)):
             for m in ms:
                 residual_part(b, z, m)
 
-        first, second, third, fourth = halves
-        add_unit(0, *first)
-        prepare_vectors()
-        gather(0, 0, range(0, TILES), 0)
-        square_unit(0, *first)
-        add_unit(0, *second)
-        reduce(0, 0, range(0, TILES), 0)
-        gather(0, 0, range(TILES, RUN), 0)
-        gather(0, 0, range(0, TILES), 1)
-        square_unit(0, *second)
-        add_unit(0, *third)
-        reduce(0, 0, range(0, TILES), 1)
-        gather(0, 0, range(TILES, RUN), 1)
-        turn_half(*third)
-        add_unit(0, *fourth)
-        reduce(0, 0, range(TILES, RUN), 0)
-        reduce(0, 0, range(TILES, RUN), 1)
-        sum_half(*third)
-        turn_half(*fourth)
-        sum_half(*fourth)
-        deviation(0)
-        for h in range(2):
-            transpose_weights(h)
-        scale_factors(0)
-        add_unit(1, *first)
-        quantise_weights()
-        residuals(0, 0, (0, 1))
-        square_unit(1, *first)
-        residuals(0, 0, (2, 3))
-        turn_chunk(0, 0)
-        scale_chunk(0, 0)
-        group_chunk(0, 0)
-        for k, (z, h) in enumerate(halves):
-            if h == 1:
-                for kind in range(2):
-                    gather(1, z, whole, kind)
-            if k + 1 < CHUNKS:
-                add_unit(1, *halves[k + 1])
-            if k > 0:
-                finish_chunk(0, k - 1)
-            quantise_chunk(0, k)
-            if h == 1:
-                for kind in range(2):
-                    reduce(1, z, whole, kind)
-            if k + 1 < CHUNKS:
-                turn_chunk(0, k + 1)
-            project_chunk(0, k)
-            if k + 1 < CHUNKS:
-                scale_chunk(0, k + 1)
-                group_chunk(0, k + 1)
-                square_unit(1, *halves[k + 1])
-            if k in (0, 1):
-                residuals(0, 1, (2 * k, 2 * k + 1))
-            if k in (2, 3):
-                residuals(1, 0, (2 * k - 4, 2 * k - 3))
-            if k == 2:
-                load_x(1, 1)
-        deviation(1)
-        turn_chunk(1, 0)
-        finish_chunk(0, CHUNKS - 1)
-        scale_factors(1)
-        scale_chunk(1, 0)
-        group_chunk(1, 0)
-        for k, (z, h) in enumerate(halves):
-            if k > 0:
-                finish_chunk(1, k - 1)
-            if k + 1 < CHUNKS:
-                turn_chunk(1, k + 1)
-                scale_chunk(1, k + 1)
-                group_chunk(1, k + 1)
-            quantise_chunk(1, k)
-            project_chunk(1, k)
-            if k in (0, 1):
-                residuals(1, 1, (2 * k, 2 * k + 1))
-        finish_chunk(1, CHUNKS - 1)
+        with tc.manual_schedule(engines=engines):
+            open_sums(0, 3)
+            add_unit(0, 0, 0)
+            square_unit(0, 0, 0)
+            add_unit(0, 0, 1)
+            prepare_vectors()
+            square_unit(0, 0, 1)
+            gather(0, 0, whole, 0)
+            for n in range(NH):
+                add_unit(0, 1, 0, (n,))
+                add_unit(0, 1, 1, (n,))
+            square_unit(0, 1, 0)
+            gather(0, 0, whole, 1)
+            reduce(0, 0, whole, 0, 0)
+            reduce(0, 0, whole, 1, 0)
+            turn_half(1, 1)
+            gather(0, 1, low, 0)
+            for kind in range(2):
+                sum_half(1, 1, kind, 2)
+            gather(0, 1, low, 1)
+            reduce(0, 1, low, 0, 1)
+            reduce(0, 1, low, 1, 1)
+            deviation(0)
+            turn_chunk(0, 0)
+            for h in range(2):
+                transpose_weights(h)
+            scale_factors(0)
+            open_sums(1, PARTS)
+            add_unit(1, 0, 0)
+            quantise_weights()
+            residuals(0, 0)
+            scale_chunk(0, 0)
+            turn_chunk(0, 1)
+            scale_chunk(0, 1)
+            group_chunk(0, 1)
+            quantise_chunk(0, 0)
+            project_chunk(0, 0)
+            add_unit(1, 0, 1)
+            square_unit(1, 0, 0)
+            square_unit(1, 0, 1)
+            gather(1, 0, whole, 0)
+            finish_chunk(0, 0)
+            quantise_chunk(0, 1)
+            project_chunk(0, 1)
+            gather(1, 0, whole, 1)
+            residuals(0, 1)
+            add_unit(1, 1, 0)
+            square_unit(1, 1, 0)
+            reduce(1, 0, whole, 0, 0)
+            turn_chunk(0, 2)
+            add_unit(1, 1, 1)
+            square_unit(1, 1, 1)
+            finish_chunk(0, 1)
+            reduce(1, 0, whole, 1, 0)
+            scale_chunk(0, 2)
+            gather(1, 1, whole, 0)
+            turn_chunk(0, 3)
+            scale_chunk(0, 3)
+            group_chunk(0, 3)
+            residuals(1, 0, (0,))
+            quantise_chunk(0, 2)
+            project_chunk(0, 2)
+            gather(1, 1, whole, 1)
+            reduce(1, 1, whole, 0, 1)
+            finish_chunk(0, 2)
+            reduce(1, 1, whole, 1, 1)
+            deviation(1)
+            quantise_chunk(0, 3)
+            project_chunk(0, 3)
+            load_x(1, 1)
+            residuals(1, 0, (1,))
+            scale_factors(1)
+            for z in range(PARTS):
+                even, odd = CPP * z, CPP * z + 1
+                turn_chunk(1, odd)
+                turn_chunk(1, even)
+                scale_chunk(1, odd)
+                group_chunk(1, odd)
+                if z == 0:
+                    finish_chunk(0, CHUNKS - 1)
+                    residuals(1, 0, (2, 3))
+                else:
+                    finish_chunk(1, even - 1)
+                    residuals(1, 1)
+                scale_chunk(1, even)
+                quantise_chunk(1, even)
+                project_chunk(1, even)
+                quantise_chunk(1, odd)
+                finish_chunk(1, even)
+                project_chunk(1, odd)
+            finish_chunk(1, CHUNKS - 1)

@@ -30,6 +30,7 @@ TILES = CHUNK // P
 OT = HD // P
 QUART = P // NH
 EPS = 1e-8
+SPLIT = ((1, 1),)
 MIXERS = ("VSVS", "VSVS")
 RESIDUALS = "SSSS"
 
@@ -41,17 +42,20 @@ def tile_axialattentionblock_pb_t_kernel(tc, xx, xy, x, norm2_w, out_w, out_b, g
     by_partition = "b n (z hp) (wp i) c -> b z n (hp wp) i c"
     xx_v = xx.rearrange(by_partition, z=PARTS, i=RUN)
     xy_v = xy.rearrange(by_partition, z=PARTS, i=RUN)
+    by_chunk = "b n (g hp) (wp i) c -> b g n (hp wp) i c"
+    xx_c = xx.rearrange(by_chunk, g=CHUNKS, i=TILES)
+    xy_c = xy.rearrange(by_chunk, g=CHUNKS, i=TILES)
     x_v = x.rearrange("b (m p) h w -> b m p (h w)", p=P)
     out_v = out.rearrange("b (m p) h w -> b m p (h w)", p=P)
 
     with ExitStack() as ctx:
         const = ctx.enter_context(tc.tile_pool(name="const", bufs=1))
-        stream = ctx.enter_context(tc.tile_pool(name="stream", bufs=3))
+        stream = ctx.enter_context(tc.tile_pool(name="stream", bufs=2))
         xpool = ctx.enter_context(tc.tile_pool(name="xpool", bufs=3 * OT))
         respool = ctx.enter_context(tc.tile_pool(name="respool", bufs=8))
         sums_pool = ctx.enter_context(tc.tile_pool(name="sums", bufs=2))
-        spool = ctx.enter_context(tc.tile_pool(name="spool", bufs=B * PARTS))
-        junk = ctx.enter_context(tc.tile_pool(name="junk", bufs=1))
+        spool = ctx.enter_context(tc.tile_pool(name="spool", bufs=3))
+        junk = ctx.enter_context(tc.tile_pool(name="junk", bufs=4))
         work = ctx.enter_context(tc.tile_pool(name="work", bufs=2))
         psum = ctx.enter_context(tc.psum_pool(name="psum", bufs=6))
 
@@ -74,8 +78,9 @@ def tile_axialattentionblock_pb_t_kernel(tc, xx, xy, x, norm2_w, out_w, out_b, g
             for k in range(pieces):
                 run = slice(k * RUN // pieces, (k + 1) * RUN // pieces)
                 for n in range(NH):
-                    for t_sb, view in zip(tiles, (xx_v, xy_v)):
-                        nc.sync.dma_start(out=t_sb[:, n, run], in_=view[b, z, n][:, run])
+                    for t_sb, view, view_c in zip(tiles, (xx_v, xy_v), (xx_c, xy_c)):
+                        src = view_c[b, CPP * z + k, n] if (b, z) in SPLIT else view[b, z, n][:, run]
+                        nc.sync.dma_start(out=t_sb[:, n, run], in_=src)
             stream_of[(b, z)] = tiles
 
         x_of = {}
@@ -98,7 +103,7 @@ def tile_axialattentionblock_pb_t_kernel(tc, xx, xy, x, norm2_w, out_w, out_b, g
         nc.sync.dma_start(out=w_rows[:], in_=out_w.rearrange("(m p) j -> p m j", p=P))
         load_part(1, 0)
         load_x(0, 0)
-        load_part(1, 1)
+        load_part(1, 1, CPP)
         load_x(0, 1)
         load_x(1, 0)
 
@@ -107,9 +112,12 @@ def tile_axialattentionblock_pb_t_kernel(tc, xx, xy, x, norm2_w, out_w, out_b, g
         half_w = const.tile([P, T], F32)
         bias_gamma = const.tile([P, OT], F32)
 
-        def prepare_vectors():
-            vec_ps = psum.tile([P, P], BF16, tag="bank")
+        vec_ps = psum.tile([P, P], BF16, tag="stat", bufs=2)
+
+        def turn_vectors():
             nc.tensor.transpose(vec_ps[:], vec_rows[:], ident_bf[:])
+
+        def prepare_vectors():
             nc.vector.tensor_copy(out=vecs[:], in_=vec_ps[:, 0 : 2 * OT])
             nc.vector.tensor_scalar_mul(out=half_w[:], in0=norm_rows[:], scalar1=0.5)
             nc.vector.tensor_tensor(out=bias_gamma[:], in0=vecs[:, 0:OT], in1=gamma, op=ALU.mult)
@@ -145,6 +153,7 @@ def tile_axialattentionblock_pb_t_kernel(tc, xx, xy, x, norm2_w, out_w, out_b, g
         r_of = {}
         res_of = {}
         tiles_of = {}
+        sT_of = {}
         scaled_of = {}
         grouped_of = {}
         codes_of = {}
@@ -201,15 +210,27 @@ def tile_axialattentionblock_pb_t_kernel(tc, xx, xy, x, norm2_w, out_w, out_b, g
                     turn(bank[:, i], s_of[(0, z)][:, h * TILES + i, t])
                 stat_banks[(z, h, t)] = bank
 
-        def sum_half(z, h, kind, slot, slots=range(T)):
+        def leave_half(z, h, engine, slots=range(T)):
+            g = z * CPP + h
+            if g not in sT_of:
+                sT_of[g] = spool.tile([P, T, CHUNK], F32, tag="sT", bufs=CHUNKS, name="sT%d" % g)
             for t in slots:
                 bank = stat_banks[(z, h, t)][:].rearrange("c i p -> c (i p)")
-                sums = partial_of[(0, kind)][:, t, slot : slot + 1]
-                if kind == 0:
-                    nc.vector.tensor_reduce(out=sums, in_=bank, axis=AX.X, op=ALU.add)
+                total = partial_of[(0, 0)][:, t, g : g + 1]
+                if engine == "S":
+                    nc.scalar.activation(out=sT_of[g][:, t], in_=bank, func=ACT.Identity, accum_out=total)
                 else:
-                    squares = junk.tile([P, CHUNK], BF16, tag="scrap_squares")
-                    nc.scalar.activation(out=squares[:], in_=bank, func=ACT.Square, accum_out=sums)
+                    nc.vector.tensor_scalar(
+                        out=sT_of[g][:, t], in0=bank, scalar1=1.0, scalar2=0.0, op0=ALU.mult, op1=ALU.add, accum_out=total
+                    )
+
+        def square_half(z, h, slots=range(T)):
+            g = z * CPP + h
+            for t in slots:
+                scrap = junk.tile([P, CHUNK], BF16, tag="scrap")
+                nc.scalar.activation(
+                    out=scrap[:], in_=sT_of[g][:, t], func=ACT.Square, accum_out=partial_of[(0, 1)][:, t, g : g + 1]
+                )
 
         def deviation(b):
             sum_s = sums_pool.tile([P, T], F32, tag="sum_s")
@@ -250,6 +271,8 @@ def tile_axialattentionblock_pb_t_kernel(tc, xx, xy, x, norm2_w, out_w, out_b, g
             res_of[(b, z, m)] = res
 
         def turn_chunk(b, g, ks=range(TILES)):
+            if b == 0:
+                return
             z, h = divmod(g, CPP)
             banks = tiles_of.setdefault((b, g), {})
             for k in ks:
@@ -266,6 +289,14 @@ def tile_axialattentionblock_pb_t_kernel(tc, xx, xy, x, norm2_w, out_w, out_b, g
                         [P, CHUNK, T], BF16, tag="grouped", bufs=3, align_bytes=64, name="grouped%d%d" % (b, g)
                     )
                 grouped = grouped_of[(b, g)]
+                if b == 0:
+                    nc.vector.tensor_tensor(
+                        out=grouped[:],
+                        in0=sT_of[g][:].rearrange("c t p -> c p t"),
+                        in1=r_of[b][:].unsqueeze(1).to_broadcast([P, CHUNK, T]),
+                        op=ALU.mult,
+                    )
+                    return
                 for i in ks:
                     nc.vector.tensor_tensor(
                         out=grouped[:, i * P : (i + 1) * P],
@@ -280,7 +311,7 @@ def tile_axialattentionblock_pb_t_kernel(tc, xx, xy, x, norm2_w, out_w, out_b, g
             for t in ks:
                 nc.scalar.activation(
                     out=scaled[:, t],
-                    in_=tiles_of[(b, g)][t][:].rearrange("c i p -> c (i p)"),
+                    in_=sT_of[g][:, t] if b == 0 else tiles_of[(b, g)][t][:].rearrange("c i p -> c (i p)"),
                     func=ACT.Copy,
                     scale=r_of[b][:, t : t + 1],
                 )
@@ -322,7 +353,12 @@ def tile_axialattentionblock_pb_t_kernel(tc, xx, xy, x, norm2_w, out_w, out_b, g
         def finish_chunk(b, g, ms=range(OT)):
             z, h = divmod(g, CPP)
             for m in ms:
-                res = res_of[(b, z, m)][:].rearrange("o (p r) -> o p r", r=RUN)[:, :, h * TILES : (h + 1) * TILES]
+                if (b, z) in SPLIT:
+                    cols = slice(h * CHUNK, (h + 1) * CHUNK)
+                    res = res_of[(b, z, m)][:, cols].rearrange("o (p r) -> o p r", r=TILES)
+                else:
+                    cols = slice(0, PART)
+                    res = res_of[(b, z, m)][:].rearrange("o (p r) -> o p r", r=RUN)[:, :, h * TILES : (h + 1) * TILES]
                 nc.vector.scalar_tensor_tensor(
                     out=res,
                     in0=acc_of[(b, g)][m][:].rearrange("o (i p) -> o p i", i=TILES),
@@ -331,8 +367,9 @@ def tile_axialattentionblock_pb_t_kernel(tc, xx, xy, x, norm2_w, out_w, out_b, g
                     op0=ALU.mult,
                     op1=ALU.add,
                 )
-                if h == CPP - 1:
-                    nc.sync.dma_start(out=out_v[b, m][:, z * PART : (z + 1) * PART], in_=res_of[(b, z, m)][:])
+                if (b, z) in SPLIT or h == CPP - 1:
+                    out_cols = slice(z * PART + cols.start, z * PART + cols.stop)
+                    nc.sync.dma_start(out=out_v[b, m][:, out_cols], in_=res_of[(b, z, m)][:, cols])
         whole, low = range(RUN), range(TILES)
         engines = {mybir.EngineType.PE, mybir.EngineType.Activation, mybir.EngineType.DVE, mybir.EngineType.Pool}
 
@@ -341,27 +378,33 @@ def tile_axialattentionblock_pb_t_kernel(tc, xx, xy, x, norm2_w, out_w, out_b, g
                 residual_part(b, z, m)
 
         with tc.manual_schedule(engines=engines):
-            open_sums(0, 3)
+            open_sums(0, CHUNKS)
             add_unit(0, 0, 0)
-            square_unit(0, 0, 0)
+            turn_half(0, 0)
+            leave_half(0, 0, "S", (0, 1))
+            for t in range(2, T):
+                square_half(0, 0, (t - 2,))
+                leave_half(0, 0, "S", (t,))
+            square_half(0, 0, (2, 3))
             add_unit(0, 0, 1)
-            prepare_vectors()
-            square_unit(0, 0, 1)
-            gather(0, 0, whole, 0)
-            for n in range(NH):
+            turn_half(0, 1)
+            turn_vectors()
+            for n in range(2):
                 add_unit(0, 1, 0, (n,))
                 add_unit(0, 1, 1, (n,))
-            square_unit(0, 1, 0)
-            gather(0, 0, whole, 1)
-            reduce(0, 0, whole, 0, 0)
-            reduce(0, 0, whole, 1, 0)
+            leave_half(0, 1, "S", (0, 1))
+            leave_half(0, 1, "V", (2, 3))
+            square_half(0, 1)
+            for n in range(2, NH):
+                add_unit(0, 1, 0, (n,))
+                add_unit(0, 1, 1, (n,))
+            turn_half(1, 0)
+            leave_half(1, 0, "V")
+            square_half(1, 0)
             turn_half(1, 1)
-            gather(0, 1, low, 0)
-            for kind in range(2):
-                sum_half(1, 1, kind, 2)
-            gather(0, 1, low, 1)
-            reduce(0, 1, low, 0, 1)
-            reduce(0, 1, low, 1, 1)
+            leave_half(1, 1, "V")
+            square_half(1, 1)
+            prepare_vectors()
             deviation(0)
             turn_chunk(0, 0)
             for h in range(2):
@@ -385,13 +428,14 @@ def tile_axialattentionblock_pb_t_kernel(tc, xx, xy, x, norm2_w, out_w, out_b, g
             quantise_chunk(0, 1)
             project_chunk(0, 1)
             gather(1, 0, whole, 1)
-            residuals(0, 1)
+            residuals(0, 1, (0,))
             add_unit(1, 1, 0)
             square_unit(1, 1, 0)
             reduce(1, 0, whole, 0, 0)
             turn_chunk(0, 2)
             add_unit(1, 1, 1)
             square_unit(1, 1, 1)
+            residuals(0, 1, (1,))
             finish_chunk(0, 1)
             reduce(1, 0, whole, 1, 0)
             scale_chunk(0, 2)
@@ -399,35 +443,42 @@ def tile_axialattentionblock_pb_t_kernel(tc, xx, xy, x, norm2_w, out_w, out_b, g
             turn_chunk(0, 3)
             scale_chunk(0, 3)
             group_chunk(0, 3)
-            residuals(1, 0, (0,))
             quantise_chunk(0, 2)
-            project_chunk(0, 2)
             gather(1, 1, whole, 1)
+            project_chunk(0, 2)
             reduce(1, 1, whole, 0, 1)
-            finish_chunk(0, 2)
             reduce(1, 1, whole, 1, 1)
             deviation(1)
-            quantise_chunk(0, 3)
-            project_chunk(0, 3)
-            load_x(1, 1)
-            residuals(1, 0, (1,))
+            residuals(0, 1, (2, 3))
+            finish_chunk(0, 2, (0, 1))
             scale_factors(1)
-            for z in range(PARTS):
-                even, odd = CPP * z, CPP * z + 1
-                turn_chunk(1, odd)
-                turn_chunk(1, even)
-                scale_chunk(1, odd)
-                group_chunk(1, odd)
-                if z == 0:
-                    finish_chunk(0, CHUNKS - 1)
-                    residuals(1, 0, (2, 3))
-                else:
-                    finish_chunk(1, even - 1)
-                    residuals(1, 1)
-                scale_chunk(1, even)
-                quantise_chunk(1, even)
-                project_chunk(1, even)
-                quantise_chunk(1, odd)
-                finish_chunk(1, even)
-                project_chunk(1, odd)
-            finish_chunk(1, CHUNKS - 1)
+            quantise_chunk(0, 3)
+            turn_chunk(1, 1)
+            project_chunk(0, 3)
+            finish_chunk(0, 2, (2, 3))
+            load_x(1, 1)
+            turn_chunk(1, 0)
+            scale_chunk(1, 1)
+            group_chunk(1, 1)
+            finish_chunk(0, 3)
+            residuals(1, 0)
+            scale_chunk(1, 0)
+            quantise_chunk(1, 0)
+            project_chunk(1, 0)
+            quantise_chunk(1, 1)
+            residuals(1, 1, (0, 1))
+            finish_chunk(1, 0)
+            project_chunk(1, 1)
+            turn_chunk(1, 3)
+            turn_chunk(1, 2)
+            scale_chunk(1, 3)
+            group_chunk(1, 3)
+            finish_chunk(1, 1)
+            residuals(1, 1, (2, 3))
+            scale_chunk(1, 2)
+            quantise_chunk(1, 2)
+            project_chunk(1, 2)
+            quantise_chunk(1, 3)
+            finish_chunk(1, 2)
+            project_chunk(1, 3)
+            finish_chunk(1, 3)

@@ -32,7 +32,6 @@ QUART = P // NH
 EPS = 1e-8
 SPLIT = ((1, 1),)
 MIXERS = ("VSVS", "VSVS")
-RESIDUALS = "SSSS"
 
 FLOPS = 2 * B * HD * HD * POS
 
@@ -71,16 +70,23 @@ def tile_axialattentionblock_pb_t_kernel(tc, xx, xy, x, norm2_w, out_w, out_b, g
 
         stream_of = {}
 
-        def load_part(b, z, pieces=1):
+        def load_part(b, z, pieces=1, heads=1):
             tiles = []
             for name in ("xx", "xy"):
                 tiles.append(stream.tile([P, NH, RUN, HEAD], BF16, tag=name, name="%s_%d_%d" % (name, b, z)))
             for k in range(pieces):
                 run = slice(k * RUN // pieces, (k + 1) * RUN // pieces)
-                for n in range(NH):
+                for n in range(0, NH, heads):
+                    group = slice(n, n + heads)
                     for t_sb, view, view_c in zip(tiles, (xx_v, xy_v), (xx_c, xy_c)):
-                        src = view_c[b, CPP * z + k, n] if (b, z) in SPLIT else view[b, z, n][:, run]
-                        nc.sync.dma_start(out=t_sb[:, n, run], in_=src)
+                        if (b, z) in SPLIT:
+                            src = view_c[b, CPP * z + k, group]
+                        else:
+                            src = view[b, z, group, :, run]
+                        nc.sync.dma_start(
+                            out=t_sb[:, group, run].rearrange("p n i c -> p n (i c)"),
+                            in_=src.rearrange("n p i c -> p n (i c)"),
+                        )
             stream_of[(b, z)] = tiles
 
         x_of = {}
@@ -99,11 +105,11 @@ def tile_axialattentionblock_pb_t_kernel(tc, xx, xy, x, norm2_w, out_w, out_b, g
         norm_rows = const.tile([P, T], BF16)
         nc.scalar.dma_start(out=norm_rows[:], in_=norm2_w.rearrange("(p t) -> p t", t=T))
         w_rows = const.tile([P, OT, HD], BF16)
-        load_part(0, 1)
+        load_part(0, 1, CPP, 2)
         nc.sync.dma_start(out=w_rows[:], in_=out_w.rearrange("(m p) j -> p m j", p=P))
         load_part(1, 0)
         load_x(0, 0)
-        load_part(1, 1, CPP)
+        load_part(1, 1, CPP, 2)
         load_x(0, 1)
         load_x(1, 0)
 
@@ -264,10 +270,7 @@ def tile_axialattentionblock_pb_t_kernel(tc, xx, xy, x, norm2_w, out_w, out_b, g
             res = respool.tile([P, PART], F32, tag="res", name="res%d%d%d" % (b, z, m))
             x_part = x_of[(b, z, m)][:]
             bias = bias_gamma[:, m : m + 1]
-            if RESIDUALS[m] == "S":
-                nc.scalar.activation(out=res[:], in_=x_part, func=ACT.Identity, bias=bias)
-            else:
-                nc.vector.tensor_scalar_add(out=res[:], in0=x_part, scalar1=bias)
+            nc.scalar.activation(out=res[:], in_=x_part, func=ACT.Identity, bias=bias)
             res_of[(b, z, m)] = res
 
         def turn_chunk(b, g, ks=range(TILES)):
@@ -389,38 +392,38 @@ def tile_axialattentionblock_pb_t_kernel(tc, xx, xy, x, norm2_w, out_w, out_b, g
             add_unit(0, 0, 1)
             turn_half(0, 1)
             turn_vectors()
-            for n in range(2):
-                add_unit(0, 1, 0, (n,))
-                add_unit(0, 1, 1, (n,))
-            leave_half(0, 1, "S", (0, 1))
-            leave_half(0, 1, "V", (2, 3))
+            add_unit(0, 1, 0, (0, 1))
+            leave_half(0, 1, "S", (0, 1, 2))
+            leave_half(0, 1, "V", (3,))
             square_half(0, 1)
-            for n in range(2, NH):
-                add_unit(0, 1, 0, (n,))
-                add_unit(0, 1, 1, (n,))
+            add_unit(0, 1, 0, (2, 3))
             turn_half(1, 0)
-            leave_half(1, 0, "V")
+            add_unit(0, 1, 1, (0, 1))
+            prepare_vectors()
+            leave_half(1, 0, "V", (0, 1))
+            add_unit(0, 1, 1, (2, 3))
+            leave_half(1, 0, "V", (2, 3))
             square_half(1, 0)
             turn_half(1, 1)
             leave_half(1, 1, "V")
             square_half(1, 1)
-            prepare_vectors()
-            deviation(0)
-            turn_chunk(0, 0)
+            add_unit(1, 0, 0, (0, 1))
             for h in range(2):
                 transpose_weights(h)
+            deviation(0)
             scale_factors(0)
             open_sums(1, PARTS)
-            add_unit(1, 0, 0)
+            add_unit(1, 0, 0, (2, 3))
             quantise_weights()
             residuals(0, 0)
             scale_chunk(0, 0)
             turn_chunk(0, 1)
             scale_chunk(0, 1)
             group_chunk(0, 1)
+            add_unit(1, 0, 1, (0,))
             quantise_chunk(0, 0)
             project_chunk(0, 0)
-            add_unit(1, 0, 1)
+            add_unit(1, 0, 1, (1, 2, 3))
             square_unit(1, 0, 0)
             square_unit(1, 0, 1)
             gather(1, 0, whole, 0)

from contextlib import ExitStack

import concourse.mybir as mybir
from concourse.masks import make_identity

F32 = mybir.dt.float32
BF16 = mybir.dt.bfloat16
U32 = mybir.dt.uint32
U8 = mybir.dt.uint8
FP8X4 = mybir.dt.float8_e4m3fn_x4
ALU = mybir.AluOpType
ACT = mybir.ActivationFunctionType
AX = mybir.AxisListType

P = 128
B = 2
NH = 4
HEAD = 128
HD = NH * HEAD
T = 4
U = 2
POS = 32 * 64
PART = 1024
PARTS = POS // PART
RUN = PART // P
CHUNK = 512
CHUNKS = POS // CHUNK
CPP = PART // CHUNK
TILES = CHUNK // P
OT = HD // P
QUART = P // NH
EPS = 1e-8
SPLIT = ((1, 1),)
MIXERS = ("VSVS", "VSVS")

FLOPS = 2 * B * HD * HD * POS


def tile_axialattentionblock_pb_t_kernel(tc, xx, xy, x, norm2_w, out_w, out_b, gamma_att, out):
    nc = tc.nc
    by_partition = "b n (z hp) (wp i) c -> b z n (hp wp) i c"
    xx_v = xx.rearrange(by_partition, z=PARTS, i=RUN)
    xy_v = xy.rearrange(by_partition, z=PARTS, i=RUN)
    by_chunk = "b n (g hp) (wp i) c -> b g n (hp wp) i c"
    xx_c = xx.rearrange(by_chunk, g=CHUNKS, i=TILES)
    xy_c = xy.rearrange(by_chunk, g=CHUNKS, i=TILES)
    x_v = x.rearrange("b (m p) h w -> b m p (h w)", p=P)
    out_v = out.rearrange("b (m p) h w -> b m p (h w)", p=P)

    with ExitStack() as ctx:
        const = ctx.enter_context(tc.tile_pool(name="const", bufs=1))
        stream = ctx.enter_context(tc.tile_pool(name="stream", bufs=2))
        xpool = ctx.enter_context(tc.tile_pool(name="xpool", bufs=3 * OT))
        respool = ctx.enter_context(tc.tile_pool(name="respool", bufs=8))
        sums_pool = ctx.enter_context(tc.tile_pool(name="sums", bufs=2))
        spool = ctx.enter_context(tc.tile_pool(name="spool", bufs=3))
        junk = ctx.enter_context(tc.tile_pool(name="junk", bufs=4))
        work = ctx.enter_context(tc.tile_pool(name="work", bufs=2))
        psum = ctx.enter_context(tc.psum_pool(name="psum", bufs=6))

        ident = const.tile([P, P], F32)
        make_identity(nc, ident[:])
        ident_bf = const.tile([P, P], BF16)
        nc.vector.tensor_copy(out=ident_bf[:], in_=ident[:])

        one = const.tile([P, 1], F32)
        nc.vector.memset(one[:], 1.0)
        one_root = const.tile([P, 1], F32)
        nc.scalar.activation(out=one_root[:], in_=one[:], func=ACT.Sqrt)

        stream_of = {}

        def load_part(b, z, pieces=1, heads=1):
            tiles = []
            for name in ("xx", "xy"):
                tiles.append(stream.tile([P, NH, RUN, HEAD], BF16, tag=name, name="%s_%d_%d" % (name, b, z)))
            for k in range(pieces):
                run = slice(k * RUN // pieces, (k + 1) * RUN // pieces)
                for n in range(0, NH, heads):
                    group = slice(n, n + heads)
                    for t_sb, view, view_c in zip(tiles, (xx_v, xy_v), (xx_c, xy_c)):
                        if (b, z) in SPLIT:
                            src = view_c[b, CPP * z + k, group]
                        else:
                            src = view[b, z, group, :, run]
                        nc.sync.dma_start(
                            out=t_sb[:, group, run].rearrange("p n i c -> p n (i c)"),
                            in_=src.rearrange("n p i c -> p n (i c)"),
                        )
            stream_of[(b, z)] = tiles

        x_of = {}

        def load_x(b, z):
            for m in range(OT):
                x_sb = xpool.tile([P, PART], BF16, tag="x", name="x_%d_%d_%d" % (b, z, m))
                nc.sync.dma_start(out=x_sb[:], in_=x_v[b, m][:, z * PART : (z + 1) * PART])
                x_of[(b, z, m)] = x_sb

        load_part(0, 0, CPP)
        vec_rows = const.tile([P, P], BF16)
        nc.vector.memset(vec_rows[:], 0.0)
        nc.scalar.dma_start(out=vec_rows[0:OT, :], in_=out_b.rearrange("(n c) -> n c", c=P))
        nc.scalar.dma_start(out=vec_rows[OT : 2 * OT, :], in_=gamma_att.rearrange("(n c) -> n c", c=P))
        norm_rows = const.tile([P, T], BF16)
        nc.scalar.dma_start(out=norm_rows[:], in_=norm2_w.rearrange("(p t) -> p t", t=T))
        w_rows = const.tile([P, OT, HD], BF16)
        load_part(0, 1, CPP, 2)
        nc.sync.dma_start(out=w_rows[:], in_=out_w.rearrange("(m p) j -> p m j", p=P))
        load_part(1, 0)
        load_x(0, 0)
        load_part(1, 1, CPP, 2)
        load_x(0, 1)
        load_x(1, 0)

        vecs = const.tile([P, 2 * OT], F32)
        gamma = vecs[:, OT : 2 * OT]
        half_w = const.tile([P, T], F32)
        bias_gamma = const.tile([P, OT], F32)

        vec_ps = psum.tile([P, P], BF16, tag="stat", bufs=2)

        def turn_vectors():
            nc.tensor.transpose(vec_ps[:], vec_rows[:], ident_bf[:])

        def prepare_vectors():
            nc.vector.tensor_copy(out=vecs[:], in_=vec_ps[:, 0 : 2 * OT])
            nc.vector.tensor_scalar_mul(out=half_w[:], in0=norm_rows[:], scalar1=0.5)
            nc.vector.tensor_tensor(out=bias_gamma[:], in0=vecs[:, 0:OT], in1=gamma, op=ALU.mult)

        w_grouped = const.tile([P, HD, T], BF16, align_bytes=64)
        w_codes = const.tile([P, HD], U32, align_bytes=64)
        w_scales = const.tile([P, HD], U8, align_bytes=64)

        def transpose_weights(h):
            words = w_rows[:].rearrange("p m j -> p (m j)").bitcast(F32)
            grouped_words = w_grouped[:].rearrange("k o t -> k (o t)").bitcast(F32)
            run = HD // 2
            wT = psum.tile([P, 2, U, P], F32, tag="bank")
            for d in range(2):
                m = 2 * h + d
                for u in range(U):
                    nc.tensor.transpose(wT[:, d, u, :], words[:, m * run + u : (m + 1) * run : 2], ident[:])
            nc.scalar.copy(
                out=grouped_words[:, h * HD : (h + 1) * HD].rearrange("k (d o u) -> k d o u", d=2, u=U),
                in_=wT[:].rearrange("k d u o -> k d o u"),
            )

        def quantise_weights():
            nc.vector.quantize_mx(
                out=w_codes[:].bitcast(FP8X4), scales=w_scales[:], in_=w_grouped[:].rearrange("k o t -> k (o t)")
            )

        s_of = {}
        squares_of = {}
        stat_banks = {}
        partial_of = {}
        std_of = {}
        r_of = {}
        res_of = {}
        tiles_of = {}
        sT_of = {}
        scaled_of = {}
        grouped_of = {}
        codes_of = {}
        acc_of = {}

        def add_unit(b, z, h, heads=range(NH)):
            if (b, z) not in s_of:
                s_of[(b, z)] = spool.tile([P, RUN, T, P], F32, tag="s", name="s%d%d" % (b, z))
            run = slice(h * TILES, (h + 1) * TILES)
            for n in heads:
                xx_n, xy_n = (t_sb[:, n, run].rearrange("p i (m t) -> p i t m", t=T) for t_sb in stream_of[(b, z)])
                nc.vector.tensor_tensor(
                    out=s_of[(b, z)][:, run, :, n * QUART : (n + 1) * QUART], in0=xx_n, in1=xy_n, op=ALU.add
                )

        def square_unit(b, z, h):
            squares = work.tile([P, TILES, T, P], F32, tag="squares", bufs=3, name="squares%d%d%d" % (b, z, h))
            nc.scalar.activation(
                out=squares[:].rearrange("p i t m -> p (i t m)"),
                in_=s_of[(b, z)][:, h * TILES : (h + 1) * TILES].rearrange("p i t m -> p (i t m)"),
                func=ACT.Square,
            )
            squares_of[(b, z, h)] = squares

        def turn(out, in_, start=True, stop=True):
            nc.tensor.matmul(out, lhsT=in_, rhs=ident[:], is_transpose=True, start=start, stop=stop)

        def gather(b, z, tiles, k, slots=range(T)):
            if (b, z, tiles.start, k) not in stat_banks:
                stat_banks[(b, z, tiles.start, k)] = psum.tile(
                    [P, T, P], F32, tag="stat", bufs=2, name="stat%d%d%d%d" % (b, z, tiles.start, k)
                )
            bank = stat_banks[(b, z, tiles.start, k)]
            for t in slots:
                for i in tiles:
                    if k == 0:
                        in_ = s_of[(b, z)][:, i, t]
                    else:
                        in_ = squares_of[(b, z, i // TILES)][:, i % TILES, t]
                    turn(bank[:, t], in_, i == tiles.start, i == tiles.stop - 1)

        def reduce(b, z, tiles, k, slot):
            bank = stat_banks[(b, z, tiles.start, k)]
            nc.vector.tensor_reduce(out=partial_of[(b, k)][:, :, slot], in_=bank[:], axis=AX.X, op=ALU.add)

        def open_sums(b, slots):
            for k in range(2):
                partial_of[(b, k)] = sums_pool.tile([P, T, slots], F32, tag="partial%d" % k, name="partial%d%d" % (b, k))

        def turn_half(z, h, slots=range(T)):
            for t in slots:
                bank = psum.tile([P, TILES, P], F32, tag="bank", name="half%d%d%d" % (z, h, t))
                for i in range(TILES):
                    turn(bank[:, i], s_of[(0, z)][:, h * TILES + i, t])
                stat_banks[(z, h, t)] = bank

        def leave_half(z, h, engine, slots=range(T)):
            g = z * CPP + h
            if g not in sT_of:
                sT_of[g] = spool.tile([P, T, CHUNK], F32, tag="sT", bufs=CHUNKS, name="sT%d" % g)
            for t in slots:
                bank = stat_banks[(z, h, t)][:].rearrange("c i p -> c (i p)")
                total = partial_of[(0, 0)][:, t, g : g + 1]
                if engine == "S":
                    nc.scalar.activation(out=sT_of[g][:, t], in_=bank, func=ACT.Identity, accum_out=total)
                else:
                    nc.vector.tensor_scalar(
                        out=sT_of[g][:, t], in0=bank, scalar1=1.0, scalar2=0.0, op0=ALU.mult, op1=ALU.add, accum_out=total
                    )

        def square_half(z, h, slots=range(T)):
            g = z * CPP + h
            for t in slots:
                scrap = junk.tile([P, CHUNK], BF16, tag="scrap")
                nc.scalar.activation(
                    out=scrap[:], in_=sT_of[g][:, t], func=ACT.Square, accum_out=partial_of[(0, 1)][:, t, g : g + 1]
                )

        def deviation(b):
            sum_s = sums_pool.tile([P, T], F32, tag="sum_s")
            nc.vector.tensor_reduce(out=sum_s[:], in_=partial_of[(b, 0)][:], axis=AX.X, op=ALU.add)
            sum_q = sums_pool.tile([P, T], F32, tag="sum_q")
            nc.vector.tensor_reduce(out=sum_q[:], in_=partial_of[(b, 1)][:], axis=AX.X, op=ALU.add)
            sum_s2 = sums_pool.tile([P, T], F32, tag="sum_s2")
            nc.vector.scalar_tensor_tensor(
                out=sum_s2[:], in0=sum_s[:], scalar=-1.0 / POS, in1=sum_s[:], op0=ALU.mult, op1=ALU.mult
            )
            centred = sums_pool.tile([P, T], F32, tag="centred")
            nc.vector.tensor_tensor(out=centred[:], in0=sum_s2[:], in1=sum_q[:], op=ALU.add)
            var = sums_pool.tile([P, T], F32, tag="var")
            nc.vector.tensor_scalar(
                out=var[:], in0=centred[:], scalar1=0.25 / (POS - 1), scalar2=0.0, op0=ALU.mult, op1=ALU.max
            )
            std = sums_pool.tile([P, T], F32, tag="std")
            nc.scalar.activation(out=std[:], in_=var[:], func=ACT.Sqrt)
            std_of[b] = std

        def scale_factors(b):
            den = sums_pool.tile([P, T], F32, tag="den")
            nc.vector.tensor_scalar_add(out=den[:], in0=std_of[b][:], scalar1=EPS)
            inv = sums_pool.tile([P, T], F32, tag="inv")
            nc.vector.reciprocal(out=inv[:], in_=den[:])
            r = sums_pool.tile([P, T], F32, tag="r")
            nc.vector.tensor_tensor(out=r[:], in0=inv[:], in1=half_w[:], op=ALU.mult)
            r_of[b] = r

        def residual_part(b, z, m):
            res = respool.tile([P, PART], F32, tag="res", name="res%d%d%d" % (b, z, m))
            x_part = x_of[(b, z, m)][:]
            bias = bias_gamma[:, m : m + 1]
            nc.scalar.activation(out=res[:], in_=x_part, func=ACT.Identity, bias=bias)
            res_of[(b, z, m)] = res

        def turn_chunk(b, g, ks=range(TILES)):
            if b == 0:
                return
            z, h = divmod(g, CPP)
            banks = tiles_of.setdefault((b, g), {})
            for k in ks:
                bank = psum.tile([P, TILES, P], F32, tag="bank", name="turn%d%d%d" % (b, g, k))
                for l in range(TILES):
                    i, t = (k, l) if MIXERS[b][g] == "V" else (l, k)
                    turn(bank[:, l], s_of[(b, z)][:, h * TILES + i, t])
                banks[k] = bank

        def scale_chunk(b, g, ks=range(TILES)):
            if MIXERS[b][g] == "V":
                if (b, g) not in grouped_of:
                    grouped_of[(b, g)] = work.tile(
                        [P, CHUNK, T], BF16, tag="grouped", bufs=3, align_bytes=64, name="grouped%d%d" % (b, g)
                    )
                grouped = grouped_of[(b, g)]
                if b == 0:
                    nc.vector.tensor_tensor(
                        out=grouped[:],
                        in0=sT_of[g][:].rearrange("c t p -> c p t"),
                        in1=r_of[b][:].unsqueeze(1).to_broadcast([P, CHUNK, T]),
                        op=ALU.mult,
                    )
                    return
                for i in ks:
                    nc.vector.tensor_tensor(
                        out=grouped[:, i * P : (i + 1) * P],
                        in0=tiles_of[(b, g)][i][:].rearrange("c t p -> c p t"),
                        in1=r_of[b][:].unsqueeze(1).to_broadcast([P, P, T]),
                        op=ALU.mult,
                    )
                return
            if (b, g) not in scaled_of:
                scaled_of[(b, g)] = work.tile([P, T, CHUNK], BF16, tag="scaled", name="scaled%d%d" % (b, g))
            scaled = scaled_of[(b, g)]
            for t in ks:
                nc.scalar.activation(
                    out=scaled[:, t],
                    in_=sT_of[g][:, t] if b == 0 else tiles_of[(b, g)][t][:].rearrange("c i p -> c (i p)"),
                    func=ACT.Copy,
                    scale=r_of[b][:, t : t + 1],
                )

        def group_chunk(b, g):
            if MIXERS[b][g] == "V":
                return
            grouped = work.tile([P, CHUNK, T], BF16, tag="grouped", bufs=3, align_bytes=64, name="grouped%d%d" % (b, g))
            nc.scalar.copy(
                out=grouped[:].rearrange("c (q i) t -> c q t i", i=4),
                in_=scaled_of[(b, g)][:].rearrange("c t (q i) -> c q t i", i=4),
            )
            grouped_of[(b, g)] = grouped

        def quantise_chunk(b, g):
            g_codes = work.tile([P, CHUNK], U32, tag="g_codes", align_bytes=64)
            g_scales = work.tile([P, CHUNK], U8, tag="g_scales", align_bytes=64)
            nc.vector.quantize_mx(
                out=g_codes[:].bitcast(FP8X4), scales=g_scales[:], in_=grouped_of[(b, g)][:].rearrange("c p t -> c (p t)")
            )
            codes_of[(b, g)] = (g_codes, g_scales)

        def project_chunk(b, g, ms=range(OT)):
            g_codes, g_scales = codes_of[(b, g)]
            accs = acc_of.setdefault((b, g), {})
            for m in ms:
                acc = psum.tile([P, CHUNK], F32, tag="bank", name="acc%d_%d_%d" % (b, g, m))
                nc.tensor.matmul_mx(
                    out=acc[:],
                    lhsT=w_codes[:, m * P : (m + 1) * P].bitcast(FP8X4),
                    lhsT_scale=w_scales[:, m * P : (m + 1) * P],
                    rhs=g_codes[:].bitcast(FP8X4),
                    rhs_scale=g_scales[:],
                    start=True,
                    stop=True,
                )
                accs[m] = acc

        def finish_chunk(b, g, ms=range(OT)):
            z, h = divmod(g, CPP)
            for m in ms:
                if (b, z) in SPLIT:
                    cols = slice(h * CHUNK, (h + 1) * CHUNK)
                    res = res_of[(b, z, m)][:, cols].rearrange("o (p r) -> o p r", r=TILES)
                else:
                    cols = slice(0, PART)
                    res = res_of[(b, z, m)][:].rearrange("o (p r) -> o p r", r=RUN)[:, :, h * TILES : (h + 1) * TILES]
                nc.vector.scalar_tensor_tensor(
                    out=res,
                    in0=acc_of[(b, g)][m][:].rearrange("o (i p) -> o p i", i=TILES),
                    scalar=gamma[:, m : m + 1],
                    in1=res,
                    op0=ALU.mult,
                    op1=ALU.add,
                )
                if (b, z) in SPLIT or h == CPP - 1:
                    out_cols = slice(z * PART + cols.start, z * PART + cols.stop)
                    nc.sync.dma_start(out=out_v[b, m][:, out_cols], in_=res_of[(b, z, m)][:, cols])
        whole, low = range(RUN), range(TILES)
        engines = {mybir.EngineType.PE, mybir.EngineType.Activation, mybir.EngineType.DVE, mybir.EngineType.Pool}

        def residuals(b, z, ms=range(OT)):
            for m in ms:
                residual_part(b, z, m)

        with tc.manual_schedule(engines=engines):
            open_sums(0, CHUNKS)
            add_unit(0, 0, 0)
            turn_half(0, 0)
            leave_half(0, 0, "S", (0, 1))
            for t in range(2, T):
                square_half(0, 0, (t - 2,))
                leave_half(0, 0, "S", (t,))
            square_half(0, 0, (2, 3))
            add_unit(0, 0, 1)
            turn_half(0, 1)
            turn_vectors()
            add_unit(0, 1, 0, (0, 1))
            leave_half(0, 1, "S", (0, 1, 2))
            leave_half(0, 1, "V", (3,))
            square_half(0, 1)
            add_unit(0, 1, 0, (2, 3))
            turn_half(1, 0)
            add_unit(0, 1, 1, (0, 1))
            prepare_vectors()
            leave_half(1, 0, "V", (0, 1))
            add_unit(0, 1, 1, (2, 3))
            leave_half(1, 0, "V", (2, 3))
            square_half(1, 0)
            turn_half(1, 1)
            leave_half(1, 1, "V")
            square_half(1, 1)
            add_unit(1, 0, 0, (0, 1))
            for h in range(2):
                transpose_weights(h)
            deviation(0)
            scale_factors(0)
            open_sums(1, PARTS)
            add_unit(1, 0, 0, (2, 3))
            quantise_weights()
            residuals(0, 0)
            scale_chunk(0, 0)
            turn_chunk(0, 1)
            scale_chunk(0, 1)
            group_chunk(0, 1)
            add_unit(1, 0, 1, (0,))
            quantise_chunk(0, 0)
            project_chunk(0, 0)
            add_unit(1, 0, 1, (1, 2, 3))
            square_unit(1, 0, 0)
            square_unit(1, 0, 1)
            gather(1, 0, whole, 0)
            finish_chunk(0, 0)
            quantise_chunk(0, 1)
            project_chunk(0, 1)
            gather(1, 0, whole, 1)
            residuals(0, 1, (0,))
            add_unit(1, 1, 0)
            square_unit(1, 1, 0)
            reduce(1, 0, whole, 0, 0)
            turn_chunk(0, 2)
            add_unit(1, 1, 1)
            square_unit(1, 1, 1)
            residuals(0, 1, (1,))
            finish_chunk(0, 1)
            reduce(1, 0, whole, 1, 0)
            scale_chunk(0, 2)
            gather(1, 1, whole, 0)
            turn_chunk(0, 3)
            scale_chunk(0, 3)
            group_chunk(0, 3)
            quantise_chunk(0, 2)
            gather(1, 1, whole, 1)
            project_chunk(0, 2)
            reduce(1, 1, whole, 0, 1)
            reduce(1, 1, whole, 1, 1)
            deviation(1)
            residuals(0, 1, (2, 3))
            finish_chunk(0, 2, (0, 1))
            scale_factors(1)
            quantise_chunk(0, 3)
            turn_chunk(1, 1)
            project_chunk(0, 3)
            finish_chunk(0, 2, (2, 3))
            load_x(1, 1)
            turn_chunk(1, 0)
            scale_chunk(1, 1)
            group_chunk(1, 1)
            finish_chunk(0, 3)
            residuals(1, 0)
            scale_chunk(1, 0)
            quantise_chunk(1, 0)
            project_chunk(1, 0)
            quantise_chunk(1, 1)
            residuals(1, 1, (0, 1))
            finish_chunk(1, 0)
            project_chunk(1, 1)
            turn_chunk(1, 3)
            turn_chunk(1, 2)
            scale_chunk(1, 3)
            group_chunk(1, 3)
            finish_chunk(1, 1)
            residuals(1, 1, (2, 3))
            scale_chunk(1, 2)
            quantise_chunk(1, 2)
            project_chunk(1, 2)
            quantise_chunk(1, 3)
            finish_chunk(1, 2)
            project_chunk(1, 3)
            finish_chunk(1, 3)
